import numpy as np
import ml_dtypes


def mxq(x, axis, fmt="e4m3"):
    dtype, down = {"e4m3": (ml_dtypes.float8_e4m3fn, 7), "e5m2": (ml_dtypes.float8_e5m2, 14)}[fmt]
    v = np.moveaxis(np.asarray(x, np.float32).astype(ml_dtypes.bfloat16).astype(np.float64), axis, -1)
    blocks = v.reshape(v.shape[:-1] + (-1, 32))
    amax = np.abs(blocks).max(-1, keepdims=True)
    byte = np.maximum(np.where(amax > 0, np.frexp(amax)[1] - 1 + 127, 0) - down, 1)
    scale = np.exp2(byte - 127.0)
    codes = (blocks / scale).astype(np.float32).astype(dtype).astype(np.float64)
    return np.moveaxis((codes * scale).reshape(v.shape), -1, axis)


WIDE = False


def mx_kscale(k):
    if not WIDE:
        return np.ones(k)
    levels = np.array([10, -10, 5, -5, 0])
    a = np.random.permutation(np.resize(levels, k // 512 * 4)).reshape(k // 512, 4)
    idx = np.arange(k)
    return np.exp2(a[idx // 512, idx % 128 // 32])


BF16 = ml_dtypes.bfloat16


def bf(x):
    return np.asarray(x, np.float32).astype(BF16)


def f64(x):
    return np.asarray(x).astype(np.float64)


B, S, HID, H, D, CHUNK = 1, 4096, 1024, 2, 128, 512
NC = S // CHUNK
MASK_VALUE = -1e9


def setup_inputs():
    s = mx_kscale(HID)
    return {"q": bf(np.random.standard_normal((B, H, S, D)) * 1.4),
            "k_scaled": bf(np.random.standard_normal((B, H, S, D)) * 1.4 / np.sqrt(D)),
            "hidden_states": bf(np.random.standard_normal((B, S, HID)) * s),
            "Wv": bf(np.random.standard_normal((HID, H * D)) / np.sqrt(HID) / s[:, None])}


def reference(q, k_scaled, hidden_states, Wv):
    q, k = f64(q), f64(k_scaled)
    v = mxq(f64(hidden_states), 2, "e4m3") @ mxq(f64(Wv), 0, "e4m3")
    v = v.reshape(B, S, H, D).transpose(0, 2, 1, 3)
    vq = mxq(v, 2, "e4m3")
    pos = np.arange(S)
    outs = []
    for n in range(NC):
        lo, mid, hi = max(n - 1, 0) * CHUNK, n * CHUNK, (n + 1) * CHUNK
        dots = q[:, :, mid:hi] @ k[:, :, lo:hi].transpose(0, 1, 3, 2)
        causal = pos[mid:hi, None] >= pos[None, lo:hi]
        dots = np.where(causal, dots, MASK_VALUE)
        e = np.exp(dots - dots.max(-1, keepdims=True))
        outs.append((mxq(e, 3, "e4m3") @ vq[:, :, lo:hi]) / e.sum(-1, keepdims=True))
    out = np.concatenate(outs, axis=2)
    return out.transpose(0, 2, 1, 3).reshape(B, S, H * D)

@@ -1,0 +1,263 @@
+from contextlib import ExitStack
+
+import concourse.mybir as mybir
+from concourse.masks import make_identity
+
+BF16 = mybir.dt.bfloat16
+F32 = mybir.dt.float32
+U32 = mybir.dt.uint32
+U8 = mybir.dt.uint8
+FP8X4 = mybir.dt.float8_e4m3fn_x4
+ALU = mybir.AluOpType
+EXP = mybir.ActivationFunctionType.Exp
+COPY = mybir.ActivationFunctionType.Copy
+ROW = mybir.AxisListType.X
+
+P = 128
+S = 4096
+HID = 1024
+H = 2
+D = 128
+CHUNK = 512
+CHUNKS = S // CHUNK
+TILES = CHUNK // P
+PASSES = HID // CHUNK
+PLANES = 2
+MASK_VALUE = -1e9
+
+FLOPS = 2 * S * HID * H * D + 2 * 2 * H * D * ((CHUNKS - 1) * CHUNK * 2 * CHUNK + CHUNK * CHUNK)
+
+
+def tile_localselfattention_pa_t_kernel(tc, q, k_scaled, hidden_states, Wv, out):
+    nc = tc.nc
+    q_rows = q.flatten_outer_dims()
+    k_rows = k_scaled.flatten_outer_dims()
+    hs_rows = hidden_states.flatten_outer_dims()
+    out_rows = out.flatten_outer_dims()
+
+    with ExitStack() as ctx:
+        const = ctx.enter_context(tc.tile_pool(name="const", bufs=1))
+        loads = ctx.enter_context(tc.tile_pool(name="loads", bufs=1))
+        keep = ctx.enter_context(tc.tile_pool(name="keep", bufs=1))
+        work = ctx.enter_context(tc.tile_pool(name="work", bufs=3))
+        small = ctx.enter_context(tc.tile_pool(name="small", bufs=4))
+        dots_psum = ctx.enter_context(tc.psum_pool(name="dots_psum", bufs=4))
+        et_psum = ctx.enter_context(tc.psum_pool(name="et_psum", bufs=1))
+        o_psum = ctx.enter_context(tc.psum_pool(name="o_psum", bufs=1))
+        prep_psum = ctx.enter_context(tc.psum_pool(name="prep_psum", bufs=2))
+
+        wv_raw = const.tile([P, PASSES, 4, H * D], BF16)
+        nc.sync.dma_start(
+            out=wv_raw[:].rearrange("p g (u e) c -> p (g u) (e c)", u=PLANES, e=2),
+            in_=Wv.rearrange("(g u p e) c -> p (g u) (e c)", g=PASSES, u=PLANES, e=2),
+        )
+        q_sb, k_sb, hs_sb = [], [], []
+        for n in range(CHUNKS):
+            k_sb.append(loads.tile([P, H, TILES, D], BF16, name="k_sb_%d" % n))
+            q_sb.append(loads.tile([P, H, TILES, D], BF16, name="q_sb_%d" % n))
+            for rows, tile_sb in ((k_rows, k_sb[n]), (q_rows, q_sb[n])):
+                for h in range(H):
+                    first = h * S + n * CHUNK
+                    nc.sync.dma_start(
+                        out=tile_sb[:, h],
+                        in_=rows[first : first + CHUNK, :].rearrange("(t p) d -> p t d", p=P),
+                    )
+            hs_sb.append(loads.tile([P, TILES, HID], BF16, name="hs_sb_%d" % n))
+            nc.sync.dma_start(
+                out=hs_sb[n][:].rearrange("p (u e) k -> p u (e k)", u=PLANES, e=2),
+                in_=hs_rows[n * CHUNK : (n + 1) * CHUNK, :].rearrange(
+                    "(u p e) k -> p u (e k)", u=PLANES, e=2
+                ),
+            )
+
+        ident_bf = const.tile([P, P], BF16)
+        make_identity(nc, ident_bf[:])
+        ident_f32 = const.tile([P, P], F32)
+        make_identity(nc, ident_f32[:])
+        causal_f32 = const.tile([P, P], F32)
+        nc.gpsimd.memset(causal_f32[:], 0.0)
+        nc.gpsimd.affine_select(
+            out=causal_f32[:],
+            in_=causal_f32[:],
+            pattern=[[-1, P]],
+            compare_op=ALU.is_ge,
+            fill=MASK_VALUE,
+            base=0,
+            channel_multiplier=1,
+        )
+        causal = const.tile([P, P], BF16)
+        nc.vector.tensor_copy(out=causal[:], in_=causal_f32[:])
+
+        e_sb = {}
+        for j in range(TILES):
+            for h in range(H):
+                e_sb[(j, h)] = keep.tile([P, 2 * CHUNK], BF16, name="e_sb_%d_%d" % (j, h))
+                if j + 1 < TILES:
+                    nc.gpsimd.memset(e_sb[(j, h)][:, CHUNK + (j + 1) * P :], 0.0)
+
+        wv_grp = const.tile([P, PASSES, H * D, 4], BF16, align_bytes=64)
+        nc.vector.tensor_copy(out=wv_grp[:], in_=wv_raw[:].rearrange("p g t c -> p g c t"))
+        wv_codes = const.tile([P, PASSES, H * D], U32, align_bytes=64)
+        wv_scales = const.tile([P, PASSES, H * D], U8, align_bytes=64)
+        nc.vector.quantize_mx(
+            out=wv_codes[:].rearrange("p g c -> p (g c)").bitcast(FP8X4),
+            scales=wv_scales[:].rearrange("p g c -> p (g c)"),
+            in_=wv_grp[:].rearrange("p g c t -> p (g c t)"),
+        )
+
+        qT = [keep.tile([P, H, CHUNK], BF16, name="qT_%d" % n) for n in range(CHUNKS)]
+        kT = [keep.tile([P, H, CHUNK], BF16, name="kT_%d" % n) for n in range(CHUNKS)]
+        v_codes = [
+            keep.tile([P, H, D], U32, align_bytes=64, name="v_codes_%d" % n) for n in range(CHUNKS)
+        ]
+        v_scales = [
+            keep.tile([P, H, D], U8, align_bytes=64, name="v_scales_%d" % n) for n in range(CHUNKS)
+        ]
+
+        def prepare(n):
+            for rows_sb, cols_sb in ((k_sb[n], kT[n]), (q_sb[n], qT[n])):
+                flipped = prep_psum.tile([P, H * TILES, P], BF16, tag="prep")
+                for h in range(H):
+                    for t in range(TILES):
+                        nc.tensor.transpose(
+                            flipped[:, h * TILES + t, :], rows_sb[:, h, t, :], ident_bf[:]
+                        )
+                nc.scalar.copy(
+                    out=cols_sb[:].rearrange("p h s -> p (h s)"),
+                    in_=flipped[:].rearrange("p a r -> p (a r)"),
+                )
+
+            hs_codes = work.tile([P, TILES, PASSES, P], U32, align_bytes=64, bufs=2)
+            hs_scales = work.tile([P, TILES, PASSES, P], U8, align_bytes=64, bufs=2)
+            for t in range(TILES):
+                hs_words = hs_sb[n][:, t, :].bitcast(F32)
+                planes = prep_psum.tile([P, PASSES * PLANES, P], F32, tag="prep")
+                for b in range(PASSES * PLANES):
+                    nc.tensor.transpose(
+                        planes[:, b, :], hs_words[:, b * P : (b + 1) * P], ident_f32[:]
+                    )
+                hs_grp = work.tile([P, PASSES * CHUNK], BF16, align_bytes=64)
+                copy_out = nc.scalar.copy if t % 2 == 0 else nc.vector.tensor_copy
+                copy_out(
+                    out=hs_grp[:].bitcast(F32).rearrange("p (g r u) -> p g r u", g=PASSES, u=PLANES),
+                    in_=planes[:].rearrange("p (g u) r -> p g r u", u=PLANES),
+                )
+                nc.vector.quantize_mx(
+                    out=hs_codes[:, t].rearrange("p g r -> p (g r)").bitcast(FP8X4),
+                    scales=hs_scales[:, t].rearrange("p g r -> p (g r)"),
+                    in_=hs_grp[:],
+                )
+
+            v_grp = work.tile([P, H, D, TILES], BF16, align_bytes=64, bufs=2)
+            for h in range(H):
+                v_ps = prep_psum.tile([P, TILES, D], F32, tag="prep")
+                for t in range(TILES):
+                    for g in range(PASSES):
+                        nc.tensor.matmul_mx(
+                            out=v_ps[:, t, :],
+                            lhsT=hs_codes[:, t, g, :].bitcast(FP8X4),
+                            lhsT_scale=hs_scales[:, t, g, :],
+                            rhs=wv_codes[:, g, h * D : (h + 1) * D].bitcast(FP8X4),
+                            rhs_scale=wv_scales[:, g, h * D : (h + 1) * D],
+                            start=(g == 0),
+                            stop=(g == PASSES - 1),
+                        )
+                nc.vector.tensor_copy(out=v_grp[:, h], in_=v_ps[:].rearrange("p t d -> p d t"))
+            nc.vector.quantize_mx(
+                out=v_codes[n][:].rearrange("p h d -> p (h d)").bitcast(FP8X4),
+                scales=v_scales[n][:].rearrange("p h d -> p (h d)"),
+                in_=v_grp[:].rearrange("p h d t -> p (h d t)"),
+            )
+
+        def attend(n, j, h, sums, o_ps):
+            first_half = 0 if n > 0 else 1
+            q_cols = qT[n][:, h, j * P : (j + 1) * P]
+            seen = (j + 1) * P
+
+            halves = []
+            if n > 0:
+                before = dots_psum.tile([P, CHUNK], F32, tag="dots")
+                nc.tensor.matmul(out=before[:], lhsT=q_cols, rhs=kT[n - 1][:, h, :], start=True, stop=True)
+                halves.append((before[:], 0))
+            own = dots_psum.tile([P, CHUNK], F32, tag="dots")
+            if j > 0:
+                nc.tensor.matmul(
+                    out=own[:, : j * P], lhsT=q_cols, rhs=kT[n][:, h, : j * P], start=True, stop=True
+                )
+            nc.tensor.matmul(
+                out=own[:, j * P : seen], lhsT=q_cols, rhs=kT[n][:, h, j * P : seen], start=True, stop=False
+            )
+            nc.tensor.matmul(out=own[:, j * P : seen], lhsT=ident_bf[:], rhs=causal[:], start=False, stop=True)
+            halves.append((own[:, :seen], CHUNK))
+
+            minus_dots = work.tile([P, 2 * CHUNK], F32)
+            lows = small.tile([P, 2], F32)
+            for i, (scores, first) in enumerate(halves):
+                nc.vector.tensor_scalar(
+                    out=minus_dots[:, first : first + scores.shape[1]],
+                    in0=scores,
+                    scalar1=-1.0,
+                    scalar2=lows[:, i - 1 : i] if i > 0 else None,
+                    op0=ALU.mult,
+                    op1=ALU.min,
+                    accum_out=lows[:, i : i + 1],
+                )
+
+            e = e_sb[(j, h)]
+            window = slice(first_half * CHUNK, CHUNK + seen)
+            nc.scalar.activation(
+                out=e[:, window],
+                in_=minus_dots[:, window],
+                func=EXP,
+                bias=lows[:, len(halves) - 1 : len(halves)],
+                scale=-1.0,
+                accum_out=sums[:, h : h + 1],
+            )
+
+            e_words = e[:].bitcast(F32)
+            eT = et_psum.tile([P, 2 * PLANES, P], F32, tag="eT")
+            for b in range(first_half * PLANES, 2 * PLANES):
+                nc.tensor.transpose(eT[:, b, :], e_words[:, b * P : (b + 1) * P], ident_f32[:])
+            e_grp = work.tile([P, 2 * CHUNK], BF16, align_bytes=64)
+            nc.scalar.copy(
+                out=e_grp[:].bitcast(F32).rearrange("p (w r u) -> p w r u", w=2, u=PLANES)[:, first_half:],
+                in_=eT[:].rearrange("p (w u) r -> p w r u", u=PLANES)[:, first_half:],
+            )
+            e_codes = work.tile([P, 2 * P], U32, align_bytes=64)
+            e_scales = work.tile([P, 2 * P], U8, align_bytes=64)
+            nc.vector.quantize_mx(
+                out=e_codes[:, first_half * P :].bitcast(FP8X4),
+                scales=e_scales[:, first_half * P :],
+                in_=e_grp[:, first_half * CHUNK :],
+            )
+            for w in range(first_half, 2):
+                nc.tensor.matmul_mx(
+                    out=o_ps[:, h, :],
+                    lhsT=e_codes[:, w * P : (w + 1) * P].bitcast(FP8X4),
+                    lhsT_scale=e_scales[:, w * P : (w + 1) * P],
+                    rhs=v_codes[n - 1 + w][:, h, :].bitcast(FP8X4),
+                    rhs_scale=v_scales[n - 1 + w][:, h, :],
+                    start=(w == first_half),
+                    stop=(w == 1),
+                )
+
+        prepare(0)
+        for n in range(CHUNKS):
+            if n + 1 < CHUNKS:
+                prepare(n + 1)
+            for j in range(TILES):
+                sums = small.tile([P, H], F32)
+                o_ps = o_psum.tile([P, H, D], F32, tag="o")
+                for h in range(H):
+                    attend(n, j, h, sums, o_ps)
+                inverse = small.tile([P, H], F32)
+                nc.vector.reciprocal(out=inverse[:], in_=sums[:])
+                o_sb = work.tile([P, H, D], F32)
+                for h in range(H):
+                    nc.scalar.activation(
+                        out=o_sb[:, h, :], in_=o_ps[:, h, :], func=COPY, scale=inverse[:, h : h + 1]
+                    )
+                first = n * CHUNK + j * P
+                nc.sync.dma_start(
+                    out=out_rows[first : first + P, :], in_=o_sb[:].rearrange("p h d -> p (h d)")
+                )

@@ -23,6 +23,8 @@ CHUNKS = S // CHUNK
 TILES = CHUNK // P
 PASSES = HID // CHUNK
 PLANES = 2
+UNITS = CHUNKS * TILES * H
+STEPS = TILES * H
 MASK_VALUE = -1e9
 
 FLOPS = 2 * S * HID * H * D + 2 * 2 * H * D * ((CHUNKS - 1) * CHUNK * 2 * CHUNK + CHUNK * CHUNK)
@@ -42,9 +44,9 @@ def tile_localselfattention_pa_t_kernel(tc, q, k_scaled, hidden_states, Wv, out)
         work = ctx.enter_context(tc.tile_pool(name="work", bufs=3))
         small = ctx.enter_context(tc.tile_pool(name="small", bufs=4))
         dots_psum = ctx.enter_context(tc.psum_pool(name="dots_psum", bufs=4))
-        et_psum = ctx.enter_context(tc.psum_pool(name="et_psum", bufs=1))
+        et_psum = ctx.enter_context(tc.psum_pool(name="et_psum", bufs=2))
         o_psum = ctx.enter_context(tc.psum_pool(name="o_psum", bufs=1))
-        prep_psum = ctx.enter_context(tc.psum_pool(name="prep_psum", bufs=2))
+        prep_psum = ctx.enter_context(tc.psum_pool(name="prep_psum", bufs=1))
 
         wv_raw = const.tile([P, PASSES, 4, H * D], BF16)
         nc.sync.dma_start(
@@ -114,66 +116,83 @@ def tile_localselfattention_pa_t_kernel(tc, q, k_scaled, hidden_states, Wv, out)
             keep.tile([P, H, D], U8, align_bytes=64, name="v_scales_%d" % n) for n in range(CHUNKS)
         ]
 
-        def prepare(n):
-            for rows_sb, cols_sb in ((k_sb[n], kT[n]), (q_sb[n], qT[n])):
-                flipped = prep_psum.tile([P, H * TILES, P], BF16, tag="prep")
-                for h in range(H):
-                    for t in range(TILES):
-                        nc.tensor.transpose(
-                            flipped[:, h * TILES + t, :], rows_sb[:, h, t, :], ident_bf[:]
-                        )
-                nc.scalar.copy(
-                    out=cols_sb[:].rearrange("p h s -> p (h s)"),
-                    in_=flipped[:].rearrange("p a r -> p (a r)"),
-                )
+        live = {}
 
-            hs_codes = work.tile([P, TILES, PASSES, P], U32, align_bytes=64, bufs=2)
-            hs_scales = work.tile([P, TILES, PASSES, P], U8, align_bytes=64, bufs=2)
-            for t in range(TILES):
-                hs_words = hs_sb[n][:, t, :].bitcast(F32)
-                planes = prep_psum.tile([P, PASSES * PLANES, P], F32, tag="prep")
-                for b in range(PASSES * PLANES):
-                    nc.tensor.transpose(
-                        planes[:, b, :], hs_words[:, b * P : (b + 1) * P], ident_f32[:]
-                    )
-                hs_grp = work.tile([P, PASSES * CHUNK], BF16, align_bytes=64)
-                copy_out = nc.scalar.copy if t % 2 == 0 else nc.vector.tensor_copy
-                copy_out(
-                    out=hs_grp[:].bitcast(F32).rearrange("p (g r u) -> p g r u", g=PASSES, u=PLANES),
-                    in_=planes[:].rearrange("p (g u) r -> p g r u", u=PLANES),
-                )
-                nc.vector.quantize_mx(
-                    out=hs_codes[:, t].rearrange("p g r -> p (g r)").bitcast(FP8X4),
-                    scales=hs_scales[:, t].rearrange("p g r -> p (g r)"),
-                    in_=hs_grp[:],
-                )
+        def hs_flip(c, t):
+            hs_words = hs_sb[c][:, t, :].bitcast(F32)
+            planes = prep_psum.tile([P, PASSES * PLANES, P], F32, tag="prep")
+            for b in range(PASSES * PLANES):
+                nc.tensor.transpose(planes[:, b, :], hs_words[:, b * P : (b + 1) * P], ident_f32[:])
+            live[("hs_planes", t)] = planes
 
-            v_grp = work.tile([P, H, D, TILES], BF16, align_bytes=64, bufs=2)
-            for h in range(H):
-                v_ps = prep_psum.tile([P, TILES, D], F32, tag="prep")
-                for t in range(TILES):
-                    for g in range(PASSES):
-                        nc.tensor.matmul_mx(
-                            out=v_ps[:, t, :],
-                            lhsT=hs_codes[:, t, g, :].bitcast(FP8X4),
-                            lhsT_scale=hs_scales[:, t, g, :],
-                            rhs=wv_codes[:, g, h * D : (h + 1) * D].bitcast(FP8X4),
-                            rhs_scale=wv_scales[:, g, h * D : (h + 1) * D],
-                            start=(g == 0),
-                            stop=(g == PASSES - 1),
-                        )
-                nc.vector.tensor_copy(out=v_grp[:, h], in_=v_ps[:].rearrange("p t d -> p d t"))
+        def hs_gather(c, t):
+            hs_grp = work.tile([P, PASSES * CHUNK], BF16, align_bytes=64)
+            copy_out = nc.scalar.copy if t % 2 == 0 else nc.vector.tensor_copy
+            copy_out(
+                out=hs_grp[:].bitcast(F32).rearrange("p (g r u) -> p g r u", g=PASSES, u=PLANES),
+                in_=live[("hs_planes", t)][:].rearrange("p (g u) r -> p g r u", u=PLANES),
+            )
+            live[("hs_grp", t)] = hs_grp
+
+        def hs_quantise(c, t):
+            if t == 0:
+                live["hs_codes"] = work.tile([P, TILES, PASSES, P], U32, align_bytes=64, bufs=2, name="hs_codes")
+                live["hs_scales"] = work.tile([P, TILES, PASSES, P], U8, align_bytes=64, bufs=2, name="hs_scales")
             nc.vector.quantize_mx(
-                out=v_codes[n][:].rearrange("p h d -> p (h d)").bitcast(FP8X4),
-                scales=v_scales[n][:].rearrange("p h d -> p (h d)"),
-                in_=v_grp[:].rearrange("p h d t -> p (h d t)"),
+                out=live["hs_codes"][:, t].rearrange("p g r -> p (g r)").bitcast(FP8X4),
+                scales=live["hs_scales"][:, t].rearrange("p g r -> p (g r)"),
+                in_=live[("hs_grp", t)][:],
             )
 
-        def attend(n, j, h, sums, o_ps):
-            first_half = 0 if n > 0 else 1
+        def qk_flip(rows_sb):
+            flipped = prep_psum.tile([P, H * TILES, P], BF16, tag="prep")
+            for h in range(H):
+                for t in range(TILES):
+                    nc.tensor.transpose(flipped[:, h * TILES + t, :], rows_sb[:, h, t, :], ident_bf[:])
+            live["flipped"] = flipped
+
+        def qk_copy(cols_sb):
+            nc.scalar.copy(
+                out=cols_sb[:].rearrange("p h s -> p (h s)"),
+                in_=live["flipped"][:].rearrange("p a r -> p (a r)"),
+            )
+
+        def v_project(c, h):
+            v_ps = prep_psum.tile([P, TILES, D], F32, tag="prep")
+            for t in range(TILES):
+                for g in range(PASSES):
+                    nc.tensor.matmul_mx(
+                        out=v_ps[:, t, :],
+                        lhsT=live["hs_codes"][:, t, g, :].bitcast(FP8X4),
+                        lhsT_scale=live["hs_scales"][:, t, g, :],
+                        rhs=wv_codes[:, g, h * D : (h + 1) * D].bitcast(FP8X4),
+                        rhs_scale=wv_scales[:, g, h * D : (h + 1) * D],
+                        start=(g == 0),
+                        stop=(g == PASSES - 1),
+                    )
+            live[("v_ps", h)] = v_ps
+
+        def v_gather(c, h):
+            if h == 0:
+                live["v_grp"] = work.tile([P, H, D, TILES], BF16, align_bytes=64, bufs=2, name="v_grp")
+            nc.vector.tensor_copy(
+                out=live["v_grp"][:, h], in_=live[("v_ps", h)][:].rearrange("p t d -> p d t")
+            )
+
+        def v_quantise(c):
+            nc.vector.quantize_mx(
+                out=v_codes[c][:].rearrange("p h d -> p (h d)").bitcast(FP8X4),
+                scales=v_scales[c][:].rearrange("p h d -> p (h d)"),
+                in_=live["v_grp"][:].rearrange("p h d t -> p (h d t)"),
+            )
+
+        def unit(u):
+            return u // STEPS, (u % STEPS) // H, u % H
+
+        def scores(u):
+            n, j, h = unit(u)
             q_cols = qT[n][:, h, j * P : (j + 1) * P]
             seen = (j + 1) * P
-
             halves = []
             if n > 0:
                 before = dots_psum.tile([P, CHUNK], F32, tag="dots")
@@ -189,50 +208,78 @@ def tile_localselfattention_pa_t_kernel(tc, q, k_scaled, hidden_states, Wv, out)
             )
             nc.tensor.matmul(out=own[:, j * P : seen], lhsT=ident_bf[:], rhs=causal[:], start=False, stop=True)
             halves.append((own[:, :seen], CHUNK))
+            live[("halves", u)] = halves
 
+        def move_scores(u):
+            halves = live[("halves", u)]
             minus_dots = work.tile([P, 2 * CHUNK], F32)
             lows = small.tile([P, 2], F32)
-            for i, (scores, first) in enumerate(halves):
+            for i, (dots, column) in enumerate(halves):
                 nc.vector.tensor_scalar(
-                    out=minus_dots[:, first : first + scores.shape[1]],
-                    in0=scores,
+                    out=minus_dots[:, column : column + dots.shape[1]],
+                    in0=dots,
                     scalar1=-1.0,
                     scalar2=lows[:, i - 1 : i] if i > 0 else None,
                     op0=ALU.mult,
                     op1=ALU.min,
                     accum_out=lows[:, i : i + 1],
                 )
+            live[("minus_dots", u)] = minus_dots
+            live[("minus_top", u)] = lows[:, len(halves) - 1 : len(halves)]
 
-            e = e_sb[(j, h)]
-            window = slice(first_half * CHUNK, CHUNK + seen)
+        def exponentials(u):
+            n, j, h = unit(u)
+            if h == 0:
+                live[("sums", n, j)] = small.tile([P, H], F32, name="sums")
+            window = slice(0 if n > 0 else CHUNK, CHUNK + (j + 1) * P)
             nc.scalar.activation(
-                out=e[:, window],
-                in_=minus_dots[:, window],
+                out=e_sb[(j, h)][:, window],
+                in_=live[("minus_dots", u)][:, window],
                 func=EXP,
-                bias=lows[:, len(halves) - 1 : len(halves)],
+                bias=live[("minus_top", u)],
                 scale=-1.0,
-                accum_out=sums[:, h : h + 1],
+                accum_out=live[("sums", n, j)][:, h : h + 1],
             )
 
-            e_words = e[:].bitcast(F32)
+        def flip_e(u):
+            n, j, h = unit(u)
+            e_words = e_sb[(j, h)][:].bitcast(F32)
             eT = et_psum.tile([P, 2 * PLANES, P], F32, tag="eT")
-            for b in range(first_half * PLANES, 2 * PLANES):
+            for b in range((0 if n > 0 else 1) * PLANES, 2 * PLANES):
                 nc.tensor.transpose(eT[:, b, :], e_words[:, b * P : (b + 1) * P], ident_f32[:])
+            live[("eT", u)] = eT
+
+        def gather_e(u):
+            n, j, h = unit(u)
+            first_half = 0 if n > 0 else 1
             e_grp = work.tile([P, 2 * CHUNK], BF16, align_bytes=64)
             nc.scalar.copy(
                 out=e_grp[:].bitcast(F32).rearrange("p (w r u) -> p w r u", w=2, u=PLANES)[:, first_half:],
-                in_=eT[:].rearrange("p (w u) r -> p w r u", u=PLANES)[:, first_half:],
+                in_=live[("eT", u)][:].rearrange("p (w u) r -> p w r u", u=PLANES)[:, first_half:],
             )
+            live[("e_grp", u)] = e_grp
+
+        def quantise_e(u):
+            n, j, h = unit(u)
+            first_half = 0 if n > 0 else 1
             e_codes = work.tile([P, 2 * P], U32, align_bytes=64)
             e_scales = work.tile([P, 2 * P], U8, align_bytes=64)
             nc.vector.quantize_mx(
                 out=e_codes[:, first_half * P :].bitcast(FP8X4),
                 scales=e_scales[:, first_half * P :],
-                in_=e_grp[:, first_half * CHUNK :],
+                in_=live[("e_grp", u)][:, first_half * CHUNK :],
             )
+            live[("e_mx", u)] = (e_codes, e_scales)
+
+        def product(u):
+            n, j, h = unit(u)
+            first_half = 0 if n > 0 else 1
+            if h == 0:
+                live[("o_ps", n, j)] = o_psum.tile([P, H, D], F32, tag="o", name="o_ps")
+            e_codes, e_scales = live[("e_mx", u)]
             for w in range(first_half, 2):
                 nc.tensor.matmul_mx(
-                    out=o_ps[:, h, :],
+                    out=live[("o_ps", n, j)][:, h, :],
                     lhsT=e_codes[:, w * P : (w + 1) * P].bitcast(FP8X4),
                     lhsT_scale=e_scales[:, w * P : (w + 1) * P],
                     rhs=v_codes[n - 1 + w][:, h, :].bitcast(FP8X4),
@@ -241,23 +288,88 @@ def tile_localselfattention_pa_t_kernel(tc, q, k_scaled, hidden_states, Wv, out)
                     stop=(w == 1),
                 )
 
-        prepare(0)
-        for n in range(CHUNKS):
-            if n + 1 < CHUNKS:
-                prepare(n + 1)
-            for j in range(TILES):
-                sums = small.tile([P, H], F32)
-                o_ps = o_psum.tile([P, H, D], F32, tag="o")
-                for h in range(H):
-                    attend(n, j, h, sums, o_ps)
-                inverse = small.tile([P, H], F32)
-                nc.vector.reciprocal(out=inverse[:], in_=sums[:])
-                o_sb = work.tile([P, H, D], F32)
-                for h in range(H):
-                    nc.scalar.activation(
-                        out=o_sb[:, h, :], in_=o_ps[:, h, :], func=COPY, scale=inverse[:, h : h + 1]
-                    )
-                first = n * CHUNK + j * P
-                nc.sync.dma_start(
-                    out=out_rows[first : first + P, :], in_=o_sb[:].rearrange("p h d -> p (h d)")
-                )
+        def inverse_sums(u):
+            n, j, h = unit(u)
+            inverse = small.tile([P, H], F32)
+            nc.vector.reciprocal(out=inverse[:], in_=live[("sums", n, j)][:])
+            live[("inverse", n, j)] = inverse
+
+        def divide_and_store(u):
+            n, j, h = unit(u)
+            o_sb = work.tile([P, H, D], F32)
+            nc.vector.tensor_tensor(
+                out=o_sb[:],
+                in0=live[("o_ps", n, j)][:],
+                in1=live[("inverse", n, j)][:].unsqueeze(2).to_broadcast([P, H, D]),
+                op=ALU.mult,
+            )
+            row = n * CHUNK + j * P
+            nc.sync.dma_start(out=out_rows[row : row + P, :], in_=o_sb[:].rearrange("p h d -> p (h d)"))
+
+        def exists(u):
+            return 0 <= u < UNITS
+
+        def step_of(i):
+            if i < 0 or i // STEPS + 1 >= CHUNKS:
+                return None, None
+            return i // STEPS + 1, i % STEPS
+
+        qk_flip(k_sb[0])
+        qk_copy(kT[0])
+        qk_flip(q_sb[0])
+        qk_copy(qT[0])
+        for t in range(TILES):
+            hs_flip(0, t)
+            hs_gather(0, t)
+            hs_quantise(0, t)
+        for h in range(H):
+            v_project(0, h)
+            v_gather(0, h)
+        v_quantise(0)
+
+        for i in range(-2, UNITS + 6):
+            c, s = step_of(i)
+            c_before, s_before = step_of(i - 1)
+
+            if c_before is not None and s_before >= 2 + TILES:
+                v_gather(c_before, s_before - 2 - TILES)
+            if c_before is not None and 2 <= s_before < 2 + TILES:
+                hs_quantise(c_before, s_before - 2)
+
+            if exists(i - 1):
+                flip_e(i - 1)
+            if c is not None and s == 0:
+                qk_flip(k_sb[c])
+            if c is not None and s == 1:
+                qk_flip(q_sb[c])
+            if c is not None and 2 <= s < 2 + TILES:
+                hs_flip(c, s - 2)
+
+            if exists(i):
+                exponentials(i)
+            if exists(i + 1):
+                move_scores(i + 1)
+            if exists(i + 2):
+                scores(i + 2)
+            if exists(i - 2):
+                gather_e(i - 2)
+            if exists(i - 3):
+                quantise_e(i - 3)
+            if exists(i - 5) and (i - 5) % H == H - 1:
+                divide_and_store(i - 5)
+
+            if c is not None and s >= 2 + TILES:
+                v_project(c, s - 2 - TILES)
+            if exists(i - 4):
+                product(i - 4)
+            if exists(i - 4) and (i - 4) % H == H - 1:
+                inverse_sums(i - 4)
+            if c_before is not None and s_before == STEPS - 1:
+                v_quantise(c_before)
+
+            if c is not None and s == 0:
+                qk_copy(kT[c])
+            if c is not None and s == 1:
+                qk_copy(qT[c])
+            if c is not None and 2 <= s < 2 + TILES:
+                hs_gather(c, s - 2)

@@ -48,11 +48,6 @@ def tile_localselfattention_pa_t_kernel(tc, q, k_scaled, hidden_states, Wv, out)
         o_psum = ctx.enter_context(tc.psum_pool(name="o_psum", bufs=1))
         prep_psum = ctx.enter_context(tc.psum_pool(name="prep_psum", bufs=1))
 
-        wv_raw = const.tile([P, PASSES, 4, H * D], BF16)
-        nc.sync.dma_start(
-            out=wv_raw[:].rearrange("p g (u e) c -> p (g u) (e c)", u=PLANES, e=2),
-            in_=Wv.rearrange("(g u p e) c -> p (g u) (e c)", g=PASSES, u=PLANES, e=2),
-        )
         q_sb, k_sb, hs_sb = [], [], []
         for n in range(CHUNKS):
             k_sb.append(loads.tile([P, H, TILES, D], BF16, name="k_sb_%d" % n))
@@ -71,6 +66,12 @@ def tile_localselfattention_pa_t_kernel(tc, q, k_scaled, hidden_states, Wv, out)
                     "(u p e) k -> p u (e k)", u=PLANES, e=2
                 ),
             )
+            if n == 0:
+                wv_raw = const.tile([P, PASSES, 4, H * D], BF16)
+                nc.sync.dma_start(
+                    out=wv_raw[:].rearrange("p g (u e) c -> p (g u) (e c)", u=PLANES, e=2),
+                    in_=Wv.rearrange("(g u p e) c -> p (g u) (e c)", g=PASSES, u=PLANES, e=2),
+                )
 
         ident_bf = const.tile([P, P], BF16)
         make_identity(nc, ident_bf[:])
@@ -118,9 +119,14 @@ def tile_localselfattention_pa_t_kernel(tc, q, k_scaled, hidden_states, Wv, out)
 
         live = {}
 
+        def prep_bank(c, shape, dtype):
+            if c == 0:
+                return dots_psum.tile(shape, dtype, tag="dots", name="prep_bank_0")
+            return prep_psum.tile(shape, dtype, tag="prep", name="prep_bank")
+
         def hs_flip(c, t):
             hs_words = hs_sb[c][:, t, :].bitcast(F32)
-            planes = prep_psum.tile([P, PASSES * PLANES, P], F32, tag="prep")
+            planes = prep_bank(c, [P, PASSES * PLANES, P], F32)
             for b in range(PASSES * PLANES):
                 nc.tensor.transpose(planes[:, b, :], hs_words[:, b * P : (b + 1) * P], ident_f32[:])
             live[("hs_planes", t)] = planes
@@ -144,8 +150,8 @@ def tile_localselfattention_pa_t_kernel(tc, q, k_scaled, hidden_states, Wv, out)
                 in_=live[("hs_grp", t)][:],
             )
 
-        def qk_flip(rows_sb):
-            flipped = prep_psum.tile([P, H * TILES, P], BF16, tag="prep")
+        def qk_flip(c, rows_sb):
+            flipped = prep_bank(c, [P, H * TILES, P], BF16)
             for h in range(H):
                 for t in range(TILES):
                     nc.tensor.transpose(flipped[:, h * TILES + t, :], rows_sb[:, h, t, :], ident_bf[:])
@@ -158,7 +164,7 @@ def tile_localselfattention_pa_t_kernel(tc, q, k_scaled, hidden_states, Wv, out)
             )
 
         def v_project(c, h):
-            v_ps = prep_psum.tile([P, TILES, D], F32, tag="prep")
+            v_ps = prep_bank(c, [P, TILES, D], F32)
             for t in range(TILES):
                 for g in range(PASSES):
                     nc.tensor.matmul_mx(
@@ -210,22 +216,25 @@ def tile_localselfattention_pa_t_kernel(tc, q, k_scaled, hidden_states, Wv, out)
             halves.append((own[:, :seen], CHUNK))
             live[("halves", u)] = halves
 
-        def move_scores(u):
+        def move_scores(u, last):
             halves = live[("halves", u)]
-            minus_dots = work.tile([P, 2 * CHUNK], F32)
-            lows = small.tile([P, 2], F32)
-            for i, (dots, column) in enumerate(halves):
-                nc.vector.tensor_scalar(
-                    out=minus_dots[:, column : column + dots.shape[1]],
-                    in0=dots,
-                    scalar1=-1.0,
-                    scalar2=lows[:, i - 1 : i] if i > 0 else None,
-                    op0=ALU.mult,
-                    op1=ALU.min,
-                    accum_out=lows[:, i : i + 1],
-                )
-            live[("minus_dots", u)] = minus_dots
-            live[("minus_top", u)] = lows[:, len(halves) - 1 : len(halves)]
+            if not last and len(halves) == 1:
+                return
+            if not last or len(halves) == 1:
+                live[("minus_dots", u)] = work.tile([P, 2 * CHUNK], F32, name="minus_dots")
+                live[("lows", u)] = small.tile([P, 2], F32, name="lows")
+            lows = live[("lows", u)]
+            dots, column = halves[-1 if last else 0]
+            nc.vector.tensor_scalar(
+                out=live[("minus_dots", u)][:, column : column + dots.shape[1]],
+                in0=dots,
+                scalar1=-1.0,
+                scalar2=lows[:, 0:1] if last and len(halves) == 2 else None,
+                op0=ALU.mult,
+                op1=ALU.min,
+                accum_out=lows[:, 1:2] if last else lows[:, 0:1],
+            )
+            live[("minus_top", u)] = lows[:, 1:2]
 
         def exponentials(u):
             n, j, h = unit(u)
@@ -314,9 +323,9 @@ def tile_localselfattention_pa_t_kernel(tc, q, k_scaled, hidden_states, Wv, out)
                 return None, None
             return i // STEPS + 1, i % STEPS
 
-        qk_flip(k_sb[0])
+        qk_flip(0, k_sb[0])
         qk_copy(kT[0])
-        qk_flip(q_sb[0])
+        qk_flip(0, q_sb[0])
         qk_copy(qT[0])
         for t in range(TILES):
             hs_flip(0, t)
@@ -339,22 +348,24 @@ def tile_localselfattention_pa_t_kernel(tc, q, k_scaled, hidden_states, Wv, out)
             if exists(i - 1):
                 flip_e(i - 1)
             if c is not None and s == 0:
-                qk_flip(k_sb[c])
+                qk_flip(c, k_sb[c])
             if c is not None and s == 1:
-                qk_flip(q_sb[c])
+                qk_flip(c, q_sb[c])
             if c is not None and 2 <= s < 2 + TILES:
                 hs_flip(c, s - 2)
 
             if exists(i):
                 exponentials(i)
             if exists(i + 1):
-                move_scores(i + 1)
+                move_scores(i + 1, last=False)
             if exists(i + 2):
                 scores(i + 2)
             if exists(i - 2):
                 gather_e(i - 2)
             if exists(i - 3):
                 quantise_e(i - 3)
+            if exists(i + 1):
+                move_scores(i + 1, last=True)
             if exists(i - 5) and (i - 5) % H == H - 1:
                 divide_and_store(i - 5)
 

@@ -10,8 +10,6 @@ U8 = mybir.dt.uint8
 FP8X4 = mybir.dt.float8_e4m3fn_x4
 ALU = mybir.AluOpType
 EXP = mybir.ActivationFunctionType.Exp
-COPY = mybir.ActivationFunctionType.Copy
-ROW = mybir.AxisListType.X
 
 P = 128
 S = 4096
@@ -23,6 +21,7 @@ CHUNKS = S // CHUNK
 TILES = CHUNK // P
 PASSES = HID // CHUNK
 PLANES = 2
+PACK = 4
 UNITS = CHUNKS * TILES * H
 STEPS = TILES * H
 MASK_VALUE = -1e9
@@ -52,12 +51,12 @@ def tile_localselfattention_pa_t_kernel(tc, q, k_scaled, hidden_states, Wv, out)
         for n in range(CHUNKS):
             k_sb.append(loads.tile([P, H, TILES, D], BF16, name="k_sb_%d" % n))
             q_sb.append(loads.tile([P, H, TILES, D], BF16, name="q_sb_%d" % n))
-            for rows, tile_sb in ((k_rows, k_sb[n]), (q_rows, q_sb[n])):
+            for rows, rows_sb in ((k_rows, k_sb[n]), (q_rows, q_sb[n])):
                 for h in range(H):
-                    first = h * S + n * CHUNK
+                    row = h * S + n * CHUNK
                     nc.sync.dma_start(
-                        out=tile_sb[:, h],
-                        in_=rows[first : first + CHUNK, :].rearrange("(t p) d -> p t d", p=P),
+                        out=rows_sb[:, h],
+                        in_=rows[row : row + CHUNK, :].rearrange("(t p) d -> p t d", p=P),
                     )
             hs_sb.append(loads.tile([P, TILES, HID], BF16, name="hs_sb_%d" % n))
             nc.sync.dma_start(
@@ -67,7 +66,7 @@ def tile_localselfattention_pa_t_kernel(tc, q, k_scaled, hidden_states, Wv, out)
                 ),
             )
             if n == 0:
-                wv_raw = const.tile([P, PASSES, 4, H * D], BF16)
+                wv_raw = const.tile([P, PASSES, PACK, H * D], BF16)
                 nc.sync.dma_start(
                     out=wv_raw[:].rearrange("p g (u e) c -> p (g u) (e c)", u=PLANES, e=2),
                     in_=Wv.rearrange("(g u p e) c -> p (g u) (e c)", g=PASSES, u=PLANES, e=2),
@@ -98,7 +97,7 @@ def tile_localselfattention_pa_t_kernel(tc, q, k_scaled, hidden_states, Wv, out)
                 if j + 1 < TILES:
                     nc.gpsimd.memset(e_sb[(j, h)][:, CHUNK + (j + 1) * P :], 0.0)
 
-        wv_grp = const.tile([P, PASSES, H * D, 4], BF16, align_bytes=64)
+        wv_grp = const.tile([P, PASSES, H * D, PACK], BF16, align_bytes=64)
         nc.vector.tensor_copy(out=wv_grp[:], in_=wv_raw[:].rearrange("p g t c -> p g c t"))
         wv_codes = const.tile([P, PASSES, H * D], U32, align_bytes=64)
         wv_scales = const.tile([P, PASSES, H * D], U8, align_bytes=64)
@@ -124,32 +123,6 @@ def tile_localselfattention_pa_t_kernel(tc, q, k_scaled, hidden_states, Wv, out)
                 return dots_psum.tile(shape, dtype, tag="dots", name="prep_bank_0")
             return prep_psum.tile(shape, dtype, tag="prep", name="prep_bank")
 
-        def hs_flip(c, t):
-            hs_words = hs_sb[c][:, t, :].bitcast(F32)
-            planes = prep_bank(c, [P, PASSES * PLANES, P], F32)
-            for b in range(PASSES * PLANES):
-                nc.tensor.transpose(planes[:, b, :], hs_words[:, b * P : (b + 1) * P], ident_f32[:])
-            live[("hs_planes", t)] = planes
-
-        def hs_gather(c, t):
-            hs_grp = work.tile([P, PASSES * CHUNK], BF16, align_bytes=64)
-            copy_out = nc.scalar.copy if t % 2 == 0 else nc.vector.tensor_copy
-            copy_out(
-                out=hs_grp[:].bitcast(F32).rearrange("p (g r u) -> p g r u", g=PASSES, u=PLANES),
-                in_=live[("hs_planes", t)][:].rearrange("p (g u) r -> p g r u", u=PLANES),
-            )
-            live[("hs_grp", t)] = hs_grp
-
-        def hs_quantise(c, t):
-            if t == 0:
-                live["hs_codes"] = work.tile([P, TILES, PASSES, P], U32, align_bytes=64, bufs=2, name="hs_codes")
-                live["hs_scales"] = work.tile([P, TILES, PASSES, P], U8, align_bytes=64, bufs=2, name="hs_scales")
-            nc.vector.quantize_mx(
-                out=live["hs_codes"][:, t].rearrange("p g r -> p (g r)").bitcast(FP8X4),
-                scales=live["hs_scales"][:, t].rearrange("p g r -> p (g r)"),
-                in_=live[("hs_grp", t)][:],
-            )
-
         def qk_flip(c, rows_sb):
             flipped = prep_bank(c, [P, H * TILES, P], BF16)
             for h in range(H):
@@ -163,33 +136,59 @@ def tile_localselfattention_pa_t_kernel(tc, q, k_scaled, hidden_states, Wv, out)
                 in_=live["flipped"][:].rearrange("p a r -> p (a r)"),
             )
 
+        hs_codes = [
+            keep.tile([P, TILES, PASSES, P], U32, align_bytes=64, name="hs_codes_%d" % i) for i in range(2)
+        ]
+        hs_scales = [
+            keep.tile([P, TILES, PASSES, P], U8, align_bytes=64, name="hs_scales_%d" % i) for i in range(2)
+        ]
+        v_grp = [keep.tile([P, H, D, PACK], BF16, align_bytes=64, name="v_grp_%d" % i) for i in range(2)]
+
+        def hs_flip(c, t):
+            hs_words = hs_sb[c][:, t, :].bitcast(F32)
+            planes = prep_bank(c, [P, PASSES * PLANES, P], F32)
+            for b in range(PASSES * PLANES):
+                nc.tensor.transpose(planes[:, b, :], hs_words[:, b * P : (b + 1) * P], ident_f32[:])
+            live["hs_planes"] = planes
+
+        def hs_gather():
+            hs_grp = work.tile([P, PASSES * CHUNK], BF16, align_bytes=64)
+            nc.scalar.copy(
+                out=hs_grp[:].bitcast(F32).rearrange("p (g r u) -> p g r u", g=PASSES, u=PLANES),
+                in_=live["hs_planes"][:].rearrange("p (g u) r -> p g r u", u=PLANES),
+            )
+            live["hs_grp"] = hs_grp
+
+        def hs_quantise(c, t):
+            nc.vector.quantize_mx(
+                out=hs_codes[c % 2][:, t].rearrange("p g r -> p (g r)").bitcast(FP8X4),
+                scales=hs_scales[c % 2][:, t].rearrange("p g r -> p (g r)"),
+                in_=live["hs_grp"][:],
+            )
+
         def v_project(c, h):
             v_ps = prep_bank(c, [P, TILES, D], F32)
             for t in range(TILES):
                 for g in range(PASSES):
                     nc.tensor.matmul_mx(
                         out=v_ps[:, t, :],
-                        lhsT=live["hs_codes"][:, t, g, :].bitcast(FP8X4),
-                        lhsT_scale=live["hs_scales"][:, t, g, :],
+                        lhsT=hs_codes[c % 2][:, t, g, :].bitcast(FP8X4),
+                        lhsT_scale=hs_scales[c % 2][:, t, g, :],
                         rhs=wv_codes[:, g, h * D : (h + 1) * D].bitcast(FP8X4),
                         rhs_scale=wv_scales[:, g, h * D : (h + 1) * D],
                         start=(g == 0),
                         stop=(g == PASSES - 1),
                     )
-            live[("v_ps", h)] = v_ps
+            live["v_ps"] = v_ps
 
         def v_gather(c, h):
-            if h == 0:
-                live["v_grp"] = work.tile([P, H, D, TILES], BF16, align_bytes=64, bufs=2, name="v_grp")
-            nc.vector.tensor_copy(
-                out=live["v_grp"][:, h], in_=live[("v_ps", h)][:].rearrange("p t d -> p d t")
-            )
+            nc.vector.tensor_copy(out=v_grp[c % 2][:, h], in_=live["v_ps"][:].rearrange("p t d -> p d t"))
 
         def v_quantise(c):
             nc.vector.quantize_mx(
                 out=v_codes[c][:].rearrange("p h d -> p (h d)").bitcast(FP8X4),
                 scales=v_scales[c][:].rearrange("p h d -> p (h d)"),
-                in_=live["v_grp"][:].rearrange("p h d t -> p (h d t)"),
+                in_=v_grp[c % 2][:].rearrange("p h d t -> p (h d t)"),
             )
 
         def unit(u):
@@ -199,11 +198,10 @@ def tile_localselfattention_pa_t_kernel(tc, q, k_scaled, hidden_states, Wv, out)
             n, j, h = unit(u)
             q_cols = qT[n][:, h, j * P : (j + 1) * P]
             seen = (j + 1) * P
-            halves = []
             if n > 0:
                 before = dots_psum.tile([P, CHUNK], F32, tag="dots")
                 nc.tensor.matmul(out=before[:], lhsT=q_cols, rhs=kT[n - 1][:, h, :], start=True, stop=True)
-                halves.append((before[:], 0))
+                live[("before", u)] = before
             own = dots_psum.tile([P, CHUNK], F32, tag="dots")
             if j > 0:
                 nc.tensor.matmul(
@@ -213,28 +211,32 @@ def tile_localselfattention_pa_t_kernel(tc, q, k_scaled, hidden_states, Wv, out)
                 out=own[:, j * P : seen], lhsT=q_cols, rhs=kT[n][:, h, j * P : seen], start=True, stop=False
             )
             nc.tensor.matmul(out=own[:, j * P : seen], lhsT=ident_bf[:], rhs=causal[:], start=False, stop=True)
-            halves.append((own[:, :seen], CHUNK))
-            live[("halves", u)] = halves
+            live[("own", u)] = own[:, :seen]
+            live[("minus_dots", u)] = work.tile([P, 2 * CHUNK], F32, name="minus_dots")
+            live[("lows", u)] = small.tile([P, 2], F32, name="lows")
 
-        def move_scores(u, last):
-            halves = live[("halves", u)]
-            if not last and len(halves) == 1:
-                return
-            if not last or len(halves) == 1:
-                live[("minus_dots", u)] = work.tile([P, 2 * CHUNK], F32, name="minus_dots")
-                live[("lows", u)] = small.tile([P, 2], F32, name="lows")
-            lows = live[("lows", u)]
-            dots, column = halves[-1 if last else 0]
+        def move_before(u):
             nc.vector.tensor_scalar(
-                out=live[("minus_dots", u)][:, column : column + dots.shape[1]],
-                in0=dots,
+                out=live[("minus_dots", u)][:, :CHUNK],
+                in0=live[("before", u)][:],
                 scalar1=-1.0,
-                scalar2=lows[:, 0:1] if last and len(halves) == 2 else None,
+                scalar2=None,
                 op0=ALU.mult,
                 op1=ALU.min,
-                accum_out=lows[:, 1:2] if last else lows[:, 0:1],
+                accum_out=live[("lows", u)][:, 0:1],
             )
-            live[("minus_top", u)] = lows[:, 1:2]
+
+        def move_own(u):
+            own = live[("own", u)]
+            nc.vector.tensor_scalar(
+                out=live[("minus_dots", u)][:, CHUNK : CHUNK + own.shape[1]],
+                in0=own,
+                scalar1=-1.0,
+                scalar2=live[("lows", u)][:, 0:1] if u >= STEPS else None,
+                op0=ALU.mult,
+                op1=ALU.min,
+                accum_out=live[("lows", u)][:, 1:2],
+            )
 
         def exponentials(u):
             n, j, h = unit(u)
@@ -245,66 +247,62 @@ def tile_localselfattention_pa_t_kernel(tc, q, k_scaled, hidden_states, Wv, out)
                 out=e_sb[(j, h)][:, window],
                 in_=live[("minus_dots", u)][:, window],
                 func=EXP,
-                bias=live[("minus_top", u)],
+                bias=live[("lows", u)][:, 1:2],
                 scale=-1.0,
                 accum_out=live[("sums", n, j)][:, h : h + 1],
             )
+
+        def first_half(u):
+            return 0 if u >= STEPS else 1
 
         def flip_e(u):
             n, j, h = unit(u)
             e_words = e_sb[(j, h)][:].bitcast(F32)
             eT = et_psum.tile([P, 2 * PLANES, P], F32, tag="eT")
-            for b in range((0 if n > 0 else 1) * PLANES, 2 * PLANES):
+            for b in range(first_half(u) * PLANES, 2 * PLANES):
                 nc.tensor.transpose(eT[:, b, :], e_words[:, b * P : (b + 1) * P], ident_f32[:])
             live[("eT", u)] = eT
 
         def gather_e(u):
-            n, j, h = unit(u)
-            first_half = 0 if n > 0 else 1
             e_grp = work.tile([P, 2 * CHUNK], BF16, align_bytes=64)
             nc.scalar.copy(
-                out=e_grp[:].bitcast(F32).rearrange("p (w r u) -> p w r u", w=2, u=PLANES)[:, first_half:],
-                in_=live[("eT", u)][:].rearrange("p (w u) r -> p w r u", u=PLANES)[:, first_half:],
+                out=e_grp[:].bitcast(F32).rearrange("p (w r u) -> p w r u", w=2, u=PLANES)[:, first_half(u) :],
+                in_=live[("eT", u)][:].rearrange("p (w u) r -> p w r u", u=PLANES)[:, first_half(u) :],
             )
             live[("e_grp", u)] = e_grp
 
         def quantise_e(u):
-            n, j, h = unit(u)
-            first_half = 0 if n > 0 else 1
             e_codes = work.tile([P, 2 * P], U32, align_bytes=64)
             e_scales = work.tile([P, 2 * P], U8, align_bytes=64)
             nc.vector.quantize_mx(
-                out=e_codes[:, first_half * P :].bitcast(FP8X4),
-                scales=e_scales[:, first_half * P :],
-                in_=live[("e_grp", u)][:, first_half * CHUNK :],
+                out=e_codes[:, first_half(u) * P :].bitcast(FP8X4),
+                scales=e_scales[:, first_half(u) * P :],
+                in_=live[("e_grp", u)][:, first_half(u) * CHUNK :],
             )
-            live[("e_mx", u)] = (e_codes, e_scales)
+            live[("e_codes", u)] = e_codes
+            live[("e_scales", u)] = e_scales
 
         def product(u):
             n, j, h = unit(u)
-            first_half = 0 if n > 0 else 1
             if h == 0:
                 live[("o_ps", n, j)] = o_psum.tile([P, H, D], F32, tag="o", name="o_ps")
-            e_codes, e_scales = live[("e_mx", u)]
-            for w in range(first_half, 2):
+            for w in range(first_half(u), 2):
                 nc.tensor.matmul_mx(
                     out=live[("o_ps", n, j)][:, h, :],
-                    lhsT=e_codes[:, w * P : (w + 1) * P].bitcast(FP8X4),
-                    lhsT_scale=e_scales[:, w * P : (w + 1) * P],
+                    lhsT=live[("e_codes", u)][:, w * P : (w + 1) * P].bitcast(FP8X4),
+                    lhsT_scale=live[("e_scales", u)][:, w * P : (w + 1) * P],
                     rhs=v_codes[n - 1 + w][:, h, :].bitcast(FP8X4),
                     rhs_scale=v_scales[n - 1 + w][:, h, :],
-                    start=(w == first_half),
+                    start=(w == first_half(u)),
                     stop=(w == 1),
                 )
 
-        def inverse_sums(u):
-            n, j, h = unit(u)
+        def invert_sums(n, j):
             inverse = small.tile([P, H], F32)
             nc.vector.reciprocal(out=inverse[:], in_=live[("sums", n, j)][:])
             live[("inverse", n, j)] = inverse
 
-        def divide_and_store(u):
-            n, j, h = unit(u)
+        def divide_and_store(n, j):
             o_sb = work.tile([P, H, D], F32)
             nc.vector.tensor_tensor(
                 out=o_sb[:],
@@ -315,12 +313,14 @@ def tile_localselfattention_pa_t_kernel(tc, q, k_scaled, hidden_states, Wv, out)
             row = n * CHUNK + j * P
             nc.sync.dma_start(out=out_rows[row : row + P, :], in_=o_sb[:].rearrange("p h d -> p (h d)"))
 
+        K_STEP, Q_STEP, HS_STEP, V_STEP = 0, 1, 2, 2 + TILES
+
         def exists(u):
             return 0 <= u < UNITS
 
         def step_of(i):
             if i < 0 or i // STEPS + 1 >= CHUNKS:
-                return None, None
+                return None, STEPS
             return i // STEPS + 1, i % STEPS
 
         qk_flip(0, k_sb[0])
@@ -329,7 +329,7 @@ def tile_localselfattention_pa_t_kernel(tc, q, k_scaled, hidden_states, Wv, out)
         qk_copy(qT[0])
         for t in range(TILES):
             hs_flip(0, t)
-            hs_gather(0, t)
+            hs_gather()
             hs_quantise(0, t)
         for h in range(H):
             v_project(0, h)
@@ -337,27 +337,27 @@ def tile_localselfattention_pa_t_kernel(tc, q, k_scaled, hidden_states, Wv, out)
         v_quantise(0)
 
         for i in range(-2, UNITS + 6):
-            c, s = step_of(i)
-            c_before, s_before = step_of(i - 1)
+            c, step = step_of(i)
+            c_before, step_before = step_of(i - 1)
 
-            if c_before is not None and s_before >= 2 + TILES:
-                v_gather(c_before, s_before - 2 - TILES)
-            if c_before is not None and 2 <= s_before < 2 + TILES:
-                hs_quantise(c_before, s_before - 2)
+            if V_STEP <= step_before < STEPS:
+                v_gather(c_before, step_before - V_STEP)
+            if HS_STEP <= step_before < V_STEP:
+                hs_quantise(c_before, step_before - HS_STEP)
 
             if exists(i - 1):
                 flip_e(i - 1)
-            if c is not None and s == 0:
+            if step == K_STEP:
                 qk_flip(c, k_sb[c])
-            if c is not None and s == 1:
+            if step == Q_STEP:
                 qk_flip(c, q_sb[c])
-            if c is not None and 2 <= s < 2 + TILES:
-                hs_flip(c, s - 2)
+            if HS_STEP <= step < V_STEP:
+                hs_flip(c, step - HS_STEP)
 
             if exists(i):
                 exponentials(i)
-            if exists(i + 1):
-                move_scores(i + 1, last=False)
+            if STEPS <= i + 1 < UNITS:
+                move_before(i + 1)
             if exists(i + 2):
                 scores(i + 2)
             if exists(i - 2):
@@ -365,22 +365,22 @@ def tile_localselfattention_pa_t_kernel(tc, q, k_scaled, hidden_states, Wv, out)
             if exists(i - 3):
                 quantise_e(i - 3)
             if exists(i + 1):
-                move_scores(i + 1, last=True)
+                move_own(i + 1)
             if exists(i - 5) and (i - 5) % H == H - 1:
-                divide_and_store(i - 5)
+                divide_and_store(*unit(i - 5)[:2])
 
-            if c is not None and s >= 2 + TILES:
-                v_project(c, s - 2 - TILES)
+            if V_STEP <= step < STEPS:
+                v_project(c, step - V_STEP)
             if exists(i - 4):
                 product(i - 4)
             if exists(i - 4) and (i - 4) % H == H - 1:
-                inverse_sums(i - 4)
-            if c_before is not None and s_before == STEPS - 1:
+                invert_sums(*unit(i - 4)[:2])
+            if step_before == STEPS - 1:
                 v_quantise(c_before)
 
-            if c is not None and s == 0:
+            if step == K_STEP:
                 qk_copy(kT[c])
-            if c is not None and s == 1:
+            if step == Q_STEP:
                 qk_copy(qT[c])
-            if c is not None and 2 <= s < 2 + TILES:
-                hs_gather(c, s - 2)
+            if HS_STEP <= step < V_STEP:
+                hs_gather()

@@ -7,6 +7,7 @@ BF16 = mybir.dt.bfloat16
 F32 = mybir.dt.float32
 U32 = mybir.dt.uint32
 U8 = mybir.dt.uint8
+I32 = mybir.dt.int32
 FP8X4 = mybir.dt.float8_e4m3fn_x4
 ALU = mybir.AluOpType
 EXP = mybir.ActivationFunctionType.Exp
@@ -23,7 +24,14 @@ PASSES = HID // CHUNK
 PLANES = 2
 PACK = 4
 UNITS = CHUNKS * TILES * H
+QUARTERS = 4
+QUADRANT = P // QUARTERS
+RUN = P // PLANES
+GROUPS = (((0, 0), (2, 0)), ((0, 1), (2, 1)), ((1, 0), (1, 1)), ((3, 0),), ((3, 1),))
+ORDER = [(g, place) for g in range(len(GROUPS)) for place in range(len(GROUPS[g]))]
+BANK_UNITS = 4
 STEPS = TILES * H
+V_WORDS = H * D
 MASK_VALUE = -1e9
 
 FLOPS = 2 * S * HID * H * D + 2 * 2 * H * D * ((CHUNKS - 1) * CHUNK * 2 * CHUNK + CHUNK * CHUNK)
@@ -42,6 +50,7 @@ def tile_localselfattention_pa_t_kernel(tc, q, k_scaled, hidden_states, Wv, out)
         keep = ctx.enter_context(tc.tile_pool(name="keep", bufs=1))
         work = ctx.enter_context(tc.tile_pool(name="work", bufs=3))
         small = ctx.enter_context(tc.tile_pool(name="small", bufs=4))
+        codes = ctx.enter_context(tc.tile_pool(name="codes", bufs=4))
         dots_psum = ctx.enter_context(tc.psum_pool(name="dots_psum", bufs=4))
         et_psum = ctx.enter_context(tc.psum_pool(name="et_psum", bufs=2))
         o_psum = ctx.enter_context(tc.psum_pool(name="o_psum", bufs=1))
@@ -60,10 +69,8 @@ def tile_localselfattention_pa_t_kernel(tc, q, k_scaled, hidden_states, Wv, out)
                     )
             hs_sb.append(loads.tile([P, TILES, HID], BF16, name="hs_sb_%d" % n))
             nc.sync.dma_start(
-                out=hs_sb[n][:].rearrange("p (u e) k -> p u (e k)", u=PLANES, e=2),
-                in_=hs_rows[n * CHUNK : (n + 1) * CHUNK, :].rearrange(
-                    "(u p e) k -> p u (e k)", u=PLANES, e=2
-                ),
+                out=hs_sb[n][:],
+                in_=hs_rows[n * CHUNK : (n + 1) * CHUNK, :].rearrange("(p t) k -> p t k", t=PACK),
             )
             if n == 0:
                 wv_raw = const.tile([P, PASSES, PACK, H * D], BF16)
@@ -88,14 +95,15 @@ def tile_localselfattention_pa_t_kernel(tc, q, k_scaled, hidden_states, Wv, out)
             channel_multiplier=1,
         )
         causal = const.tile([P, P], BF16)
-        nc.vector.tensor_copy(out=causal[:], in_=causal_f32[:])
+        nc.vector.tensor_copy(
+            out=causal[:].rearrange("p (u x e) -> p u x e", u=PLANES, e=2),
+            in_=causal_f32[:].rearrange("p (x u e) -> p u x e", u=PLANES, e=2),
+        )
 
-        e_sb = {}
-        for j in range(TILES):
-            for h in range(H):
-                e_sb[(j, h)] = keep.tile([P, 2 * CHUNK], BF16, name="e_sb_%d_%d" % (j, h))
-                if j + 1 < TILES:
-                    nc.gpsimd.memset(e_sb[(j, h)][:, CHUNK + (j + 1) * P :], 0.0)
+        e_sb = [
+            keep.tile([P, PLANES, QUARTERS * (1 + len(group)), RUN], BF16, name="e_sb_%d" % g)
+            for g, group in enumerate(GROUPS)
+        ]
 
         wv_grp = const.tile([P, PASSES, H * D, PACK], BF16, align_bytes=64)
         nc.vector.tensor_copy(out=wv_grp[:], in_=wv_raw[:].rearrange("p g t c -> p g c t"))
@@ -109,12 +117,25 @@ def tile_localselfattention_pa_t_kernel(tc, q, k_scaled, hidden_states, Wv, out)
 
         qT = [keep.tile([P, H, CHUNK], BF16, name="qT_%d" % n) for n in range(CHUNKS)]
         kT = [keep.tile([P, H, CHUNK], BF16, name="kT_%d" % n) for n in range(CHUNKS)]
-        v_codes = [
-            keep.tile([P, H, D], U32, align_bytes=64, name="v_codes_%d" % n) for n in range(CHUNKS)
+        v_mx = [
+            keep.tile([P, V_WORDS + V_WORDS // PACK], U32, align_bytes=64, name="v_mx_%d" % n)
+            for n in range(CHUNKS)
         ]
-        v_scales = [
-            keep.tile([P, H, D], U8, align_bytes=64, name="v_scales_%d" % n) for n in range(CHUNKS)
-        ]
+        v_kept, v_moved = {}, {}
+        for q in (1, 2):
+            for i in range(2):
+                v_kept[(q, i)] = keep.tile([P, V_WORDS], U32, align_bytes=64, name="v_kept_%d_%d" % (q, i))
+                v_moved[(q, i)] = keep.tile(
+                    [P, V_WORDS + V_WORDS // PACK], U32, align_bytes=64, name="v_moved_%d_%d" % (q, i)
+                )
+                nc.gpsimd.memset(v_kept[(q, i)][:].bitcast(I32), 0)
+                nc.gpsimd.memset(v_moved[(q, i)][:].bitcast(I32), 0)
+
+        def v_words(tile, h):
+            return tile[:, h * D : (h + 1) * D].bitcast(FP8X4)
+
+        def v_scale_bytes(tile, h):
+            return tile[:, V_WORDS:].bitcast(U8)[:, h * D : (h + 1) * D]
 
         live = {}
 
@@ -130,10 +151,20 @@ def tile_localselfattention_pa_t_kernel(tc, q, k_scaled, hidden_states, Wv, out)
                     nc.tensor.transpose(flipped[:, h * TILES + t, :], rows_sb[:, h, t, :], ident_bf[:])
             live["flipped"] = flipped
 
-        def qk_copy(cols_sb):
+        def q_copy(c):
             nc.scalar.copy(
-                out=cols_sb[:].rearrange("p h s -> p (h s)"),
-                in_=live["flipped"][:].rearrange("p a r -> p (a r)"),
+                out=qT[c][:].rearrange("p h s -> p (h s)").bitcast(F32),
+                in_=live["flipped"][:].rearrange("p a r -> p (a r)").bitcast(F32),
+            )
+
+        def k_copy(c):
+            nc.scalar.copy(
+                out=kT[c][:].rearrange("p h s -> p (h s)").bitcast(F32).rearrange(
+                    "p (a u x) -> p a u x", u=PLANES, x=RUN // 2
+                ),
+                in_=live["flipped"][:].rearrange("p a r -> p (a r)").bitcast(F32).rearrange(
+                    "p (a x u) -> p a u x", u=PLANES, x=RUN // 2
+                ),
             )
 
         hs_codes = [
@@ -186,13 +217,49 @@ def tile_localselfattention_pa_t_kernel(tc, q, k_scaled, hidden_states, Wv, out)
 
         def v_quantise(c):
             nc.vector.quantize_mx(
-                out=v_codes[c][:].rearrange("p h d -> p (h d)").bitcast(FP8X4),
-                scales=v_scales[c][:].rearrange("p h d -> p (h d)"),
+                out=v_mx[c][:, :V_WORDS].bitcast(FP8X4),
+                scales=v_mx[c][:, V_WORDS:].bitcast(U8),
                 in_=v_grp[c % 2][:].rearrange("p h d t -> p (h d t)"),
             )
 
+        def v_share(c):
+            for q in (1, 2):
+                kept, moved, border = v_kept[(q, c % 2)], v_moved[(q, c % 2)], q * QUADRANT
+                nc.sync.dma_start(
+                    out=kept[:border, :].bitcast(I32), in_=v_mx[c][:border, :V_WORDS].bitcast(I32)
+                )
+                nc.sync.dma_start(
+                    out=moved[border:, :].bitcast(I32), in_=v_mx[c][: P - border, :].bitcast(I32)
+                )
+
         def unit(u):
-            return u // STEPS, (u % STEPS) // H, u % H
+            g, place = ORDER[u % STEPS]
+            return (u // STEPS,) + GROUPS[g][place]
+
+        def is_second(u):
+            return ORDER[u % STEPS][1] == 1
+
+        def is_first(u):
+            g, place = ORDER[u % STEPS]
+            return place == 0 and len(GROUPS[g]) == 2
+
+        def slots(u):
+            n, j, h = unit(u)
+            own = QUARTERS + (QUARTERS - 1 - j if is_second(u) else 0)
+            first, last = own, own + j + 1
+            if n > 0 and is_second(u):
+                last += QUARTERS
+            elif n > 0:
+                first -= QUARTERS
+            return slice(first, last)
+
+        def passes(u):
+            n, j, h = unit(u)
+            if is_first(u):
+                return range(0, 1 if n > 0 else 0)
+            if is_second(u):
+                return range(1, 3 if n > 0 else 2)
+            return range(0 if n > 0 else 1, 2)
 
         def scores(u):
             n, j, h = unit(u)
@@ -212,12 +279,17 @@ def tile_localselfattention_pa_t_kernel(tc, q, k_scaled, hidden_states, Wv, out)
             )
             nc.tensor.matmul(out=own[:, j * P : seen], lhsT=ident_bf[:], rhs=causal[:], start=False, stop=True)
             live[("own", u)] = own[:, :seen]
-            live[("minus_dots", u)] = work.tile([P, 2 * CHUNK], F32, name="minus_dots")
+            minus_dots = work.tile([P, 2 * CHUNK], F32, name="minus_dots")
+            own_at = CHUNK if n > 0 and not is_second(u) else 0
+            before_at = seen if is_second(u) else 0
+            live[("minus_own", u)] = minus_dots[:, own_at : own_at + seen]
+            live[("minus_before", u)] = minus_dots[:, before_at : before_at + CHUNK]
+            live[("minus_dots", u)] = minus_dots[:, : seen + (CHUNK if n > 0 else 0)]
             live[("lows", u)] = small.tile([P, 2], F32, name="lows")
 
         def move_before(u):
             nc.vector.tensor_scalar(
-                out=live[("minus_dots", u)][:, :CHUNK],
+                out=live[("minus_before", u)],
                 in0=live[("before", u)][:],
                 scalar1=-1.0,
                 scalar2=None,
@@ -227,10 +299,9 @@ def tile_localselfattention_pa_t_kernel(tc, q, k_scaled, hidden_states, Wv, out)
             )
 
         def move_own(u):
-            own = live[("own", u)]
             nc.vector.tensor_scalar(
-                out=live[("minus_dots", u)][:, CHUNK : CHUNK + own.shape[1]],
-                in0=own,
+                out=live[("minus_own", u)],
+                in0=live[("own", u)],
                 scalar1=-1.0,
                 scalar2=live[("lows", u)][:, 0:1] if u >= STEPS else None,
                 op0=ALU.mult,
@@ -239,79 +310,95 @@ def tile_localselfattention_pa_t_kernel(tc, q, k_scaled, hidden_states, Wv, out)
             )
 
         def exponentials(u):
-            n, j, h = unit(u)
-            if h == 0:
-                live[("sums", n, j)] = small.tile([P, H], F32, name="sums")
-            window = slice(0 if n > 0 else CHUNK, CHUNK + (j + 1) * P)
+            bank, at = u // BANK_UNITS, column(u)
+            if u % BANK_UNITS == 0:
+                live[("sums", bank)] = small.tile([P, BANK_UNITS], F32, name="sums")
             nc.scalar.activation(
-                out=e_sb[(j, h)][:, window],
-                in_=live[("minus_dots", u)][:, window],
+                out=e_sb[ORDER[u % STEPS][0]][:, :, slots(u), :].rearrange("p u s x -> p s u x"),
+                in_=live[("minus_dots", u)].rearrange("p (s u x) -> p s u x", u=PLANES, x=RUN),
                 func=EXP,
                 bias=live[("lows", u)][:, 1:2],
                 scale=-1.0,
-                accum_out=live[("sums", n, j)][:, h : h + 1],
+                accum_out=live[("sums", bank)][:, at : at + 1],
             )
 
-        def first_half(u):
-            return 0 if u >= STEPS else 1
-
         def flip_e(u):
-            n, j, h = unit(u)
-            e_words = e_sb[(j, h)][:].bitcast(F32)
-            eT = et_psum.tile([P, 2 * PLANES, P], F32, tag="eT")
-            for b in range(first_half(u) * PLANES, 2 * PLANES):
-                nc.tensor.transpose(eT[:, b, :], e_words[:, b * P : (b + 1) * P], ident_f32[:])
+            e_words = e_sb[ORDER[u % STEPS][0]][:].rearrange("p u s x -> p u (s x)").bitcast(F32)
+            eT = et_psum.tile([P, 2, PLANES, P], F32, tag="eT")
+            for w, s in enumerate(passes(u)):
+                for b in range(PLANES):
+                    nc.tensor.transpose(eT[:, w, b, :], e_words[:, b, s * P : (s + 1) * P], ident_f32[:])
             live[("eT", u)] = eT
 
         def gather_e(u):
+            count = len(passes(u))
             e_grp = work.tile([P, 2 * CHUNK], BF16, align_bytes=64)
             nc.scalar.copy(
-                out=e_grp[:].bitcast(F32).rearrange("p (w r u) -> p w r u", w=2, u=PLANES)[:, first_half(u) :],
-                in_=live[("eT", u)][:].rearrange("p (w u) r -> p w r u", u=PLANES)[:, first_half(u) :],
+                out=e_grp[:, : count * CHUNK].bitcast(F32).rearrange("p (w r u) -> p w r u", w=count, u=PLANES),
+                in_=live[("eT", u)][:, :count].rearrange("p w u r -> p w r u"),
             )
             live[("e_grp", u)] = e_grp
 
         def quantise_e(u):
-            e_codes = work.tile([P, 2 * P], U32, align_bytes=64)
-            e_scales = work.tile([P, 2 * P], U8, align_bytes=64)
+            count = len(passes(u))
+            e_codes = codes.tile([P, 2 * P], U32, align_bytes=64)
+            e_scales = codes.tile([P, 2 * P], U8, align_bytes=64)
             nc.vector.quantize_mx(
-                out=e_codes[:, first_half(u) * P :].bitcast(FP8X4),
-                scales=e_scales[:, first_half(u) * P :],
-                in_=live[("e_grp", u)][:, first_half(u) * CHUNK :],
+                out=e_codes[:, : count * P].bitcast(FP8X4),
+                scales=e_scales[:, : count * P],
+                in_=live[("e_grp", u)][:, : count * CHUNK],
             )
-            live[("e_codes", u)] = e_codes
-            live[("e_scales", u)] = e_scales
+            for w, s in enumerate(passes(u)):
+                live[("e_pass", u, s)] = (e_codes[:, w * P : (w + 1) * P], e_scales[:, w * P : (w + 1) * P])
 
-        def product(u):
+        def column(u):
             n, j, h = unit(u)
-            if h == 0:
-                live[("o_ps", n, j)] = o_psum.tile([P, H, D], F32, tag="o", name="o_ps")
-            for w in range(first_half(u), 2):
+            return j // 2 * H + h
+
+        def product(u, last):
+            n, j, h = unit(u)
+            bank = u // BANK_UNITS
+            if u % BANK_UNITS == 0:
+                live[("o_ps", bank)] = o_psum.tile([P, BANK_UNITS, D], F32, tag="o", name="o_ps")
+            factors = []
+            if n > 0:
+                before = live[("e_pass", u, 2 if is_second(u) else 0)]
+                factors.append((before, (v_words(v_mx[n - 1], h), v_scale_bytes(v_mx[n - 1], h))))
+            if is_first(u):
+                v_own = (v_words(v_kept[(j + 1, n % 2)], h), v_scale_bytes(v_mx[n], h))
+            elif is_second(u):
+                moved = v_moved[(QUARTERS - 1 - j, n % 2)]
+                v_own = (v_words(moved, h), v_scale_bytes(moved, h))
+            else:
+                v_own = (v_words(v_mx[n], h), v_scale_bytes(v_mx[n], h))
+            factors.append((live[("e_pass", last, 1)], v_own))
+            for w, (e_side, v_side) in enumerate(factors):
                 nc.tensor.matmul_mx(
-                    out=live[("o_ps", n, j)][:, h, :],
-                    lhsT=live[("e_codes", u)][:, w * P : (w + 1) * P].bitcast(FP8X4),
-                    lhsT_scale=live[("e_scales", u)][:, w * P : (w + 1) * P],
-                    rhs=v_codes[n - 1 + w][:, h, :].bitcast(FP8X4),
-                    rhs_scale=v_scales[n - 1 + w][:, h, :],
-                    start=(w == first_half(u)),
-                    stop=(w == 1),
+                    out=live[("o_ps", bank)][:, column(u), :],
+                    lhsT=e_side[0].bitcast(FP8X4),
+                    lhsT_scale=e_side[1],
+                    rhs=v_side[0],
+                    rhs_scale=v_side[1],
+                    start=(w == 0),
+                    stop=(w == len(factors) - 1),
                 )
 
-        def invert_sums(n, j):
-            inverse = small.tile([P, H], F32)
-            nc.vector.reciprocal(out=inverse[:], in_=live[("sums", n, j)][:])
-            live[("inverse", n, j)] = inverse
+        def invert_sums(bank):
+            inverse = small.tile([P, BANK_UNITS], F32)
+            nc.vector.reciprocal(out=inverse[:], in_=live[("sums", bank)][:])
+            live[("inverse", bank)] = inverse
 
-        def divide_and_store(n, j):
-            o_sb = work.tile([P, H, D], F32)
+        def divide_and_store(bank):
+            o_sb = work.tile([P, BANK_UNITS, D], F32)
             nc.vector.tensor_tensor(
                 out=o_sb[:],
-                in0=live[("o_ps", n, j)][:],
-                in1=live[("inverse", n, j)][:].unsqueeze(2).to_broadcast([P, H, D]),
+                in0=live[("o_ps", bank)][:],
+                in1=live[("inverse", bank)][:].unsqueeze(2).to_broadcast([P, BANK_UNITS, D]),
                 op=ALU.mult,
             )
-            row = n * CHUNK + j * P
-            nc.sync.dma_start(out=out_rows[row : row + P, :], in_=o_sb[:].rearrange("p h d -> p (h d)"))
+            n, x = bank // 2, bank % 2
+            rows = out_rows[n * CHUNK : (n + 1) * CHUNK, :].rearrange("(a x p) c -> x p a c", a=2, x=2)
+            nc.sync.dma_start(out=rows[x], in_=o_sb[:].rearrange("p (a h) d -> p a (h d)", a=2))
 
         K_STEP, Q_STEP, HS_STEP, V_STEP = 0, 1, 2, 2 + TILES
 
@@ -324,9 +411,9 @@ def tile_localselfattention_pa_t_kernel(tc, q, k_scaled, hidden_states, Wv, out)
             return i // STEPS + 1, i % STEPS
 
         qk_flip(0, k_sb[0])
-        qk_copy(kT[0])
+        k_copy(0)
         qk_flip(0, q_sb[0])
-        qk_copy(qT[0])
+        q_copy(0)
         for t in range(TILES):
             hs_flip(0, t)
             hs_gather()
@@ -335,6 +422,7 @@ def tile_localselfattention_pa_t_kernel(tc, q, k_scaled, hidden_states, Wv, out)
             v_project(0, h)
             v_gather(0, h)
         v_quantise(0)
+        v_share(0)
 
         for i in range(-2, UNITS + 6):
             c, step = step_of(i)
@@ -345,7 +433,7 @@ def tile_localselfattention_pa_t_kernel(tc, q, k_scaled, hidden_states, Wv, out)
             if HS_STEP <= step_before < V_STEP:
                 hs_quantise(c_before, step_before - HS_STEP)
 
-            if exists(i - 1):
+            if exists(i - 1) and passes(i - 1):
                 flip_e(i - 1)
             if step == K_STEP:
                 qk_flip(c, k_sb[c])
@@ -360,27 +448,30 @@ def tile_localselfattention_pa_t_kernel(tc, q, k_scaled, hidden_states, Wv, out)
                 move_before(i + 1)
             if exists(i + 2):
                 scores(i + 2)
-            if exists(i - 2):
+            if exists(i - 2) and passes(i - 2):
                 gather_e(i - 2)
-            if exists(i - 3):
+            if exists(i - 3) and passes(i - 3):
                 quantise_e(i - 3)
             if exists(i + 1):
                 move_own(i + 1)
-            if exists(i - 5) and (i - 5) % H == H - 1:
-                divide_and_store(*unit(i - 5)[:2])
+            if exists(i - 5) and (i - 5) % BANK_UNITS == BANK_UNITS - 1:
+                divide_and_store((i - 5) // BANK_UNITS)
 
             if V_STEP <= step < STEPS:
                 v_project(c, step - V_STEP)
-            if exists(i - 4):
-                product(i - 4)
-            if exists(i - 4) and (i - 4) % H == H - 1:
-                invert_sums(*unit(i - 4)[:2])
+            if exists(i - 4) and not is_first(i - 4):
+                if is_second(i - 4):
+                    product(i - 5, i - 4)
+                product(i - 4, i - 4)
+            if exists(i - 4) and (i - 4) % BANK_UNITS == BANK_UNITS - 1:
+                invert_sums((i - 4) // BANK_UNITS)
             if step_before == STEPS - 1:
                 v_quantise(c_before)
+                v_share(c_before)
 
             if step == K_STEP:
-                qk_copy(kT[c])
+                k_copy(c)
             if step == Q_STEP:
-                qk_copy(qT[c])
+                q_copy(c)
             if HS_STEP <= step < V_STEP:
                 hs_gather()

@@ -46,7 +46,7 @@ def tile_localselfattention_pa_t_kernel(tc, q, k_scaled, hidden_states, Wv, out)
 
     with ExitStack() as ctx:
         const = ctx.enter_context(tc.tile_pool(name="const", bufs=1))
-        loads = ctx.enter_context(tc.tile_pool(name="loads", bufs=1))
+        loads = ctx.enter_context(tc.tile_pool(name="loads", bufs=2))
         keep = ctx.enter_context(tc.tile_pool(name="keep", bufs=1))
         work = ctx.enter_context(tc.tile_pool(name="work", bufs=3))
         small = ctx.enter_context(tc.tile_pool(name="small", bufs=4))
@@ -57,9 +57,10 @@ def tile_localselfattention_pa_t_kernel(tc, q, k_scaled, hidden_states, Wv, out)
         prep_psum = ctx.enter_context(tc.psum_pool(name="prep_psum", bufs=1))
 
         q_sb, k_sb, hs_sb = [], [], []
-        for n in range(CHUNKS):
-            k_sb.append(loads.tile([P, H, TILES, D], BF16, name="k_sb_%d" % n))
-            q_sb.append(loads.tile([P, H, TILES, D], BF16, name="q_sb_%d" % n))
+
+        def load(n):
+            k_sb.append(loads.tile([P, H, TILES, D], BF16, name="k_sb"))
+            q_sb.append(loads.tile([P, H, TILES, D], BF16, name="q_sb"))
             for rows, rows_sb in ((k_rows, k_sb[n]), (q_rows, q_sb[n])):
                 for h in range(H):
                     row = h * S + n * CHUNK
@@ -67,17 +68,19 @@ def tile_localselfattention_pa_t_kernel(tc, q, k_scaled, hidden_states, Wv, out)
                         out=rows_sb[:, h],
                         in_=rows[row : row + CHUNK, :].rearrange("(t p) d -> p t d", p=P),
                     )
-            hs_sb.append(loads.tile([P, TILES, HID], BF16, name="hs_sb_%d" % n))
+            hs_sb.append(loads.tile([P, TILES, HID], BF16, name="hs_sb"))
             nc.sync.dma_start(
                 out=hs_sb[n][:],
                 in_=hs_rows[n * CHUNK : (n + 1) * CHUNK, :].rearrange("(p t) k -> p t k", t=PACK),
             )
-            if n == 0:
-                wv_raw = const.tile([P, PASSES, PACK, H * D], BF16)
-                nc.sync.dma_start(
-                    out=wv_raw[:].rearrange("p g (u e) c -> p (g u) (e c)", u=PLANES, e=2),
-                    in_=Wv.rearrange("(g u p e) c -> p (g u) (e c)", g=PASSES, u=PLANES, e=2),
-                )
+
+        load(0)
+        wv_raw = const.tile([P, PASSES, PACK, H * D], BF16)
+        nc.sync.dma_start(
+            out=wv_raw[:].rearrange("p g (u e) c -> p (g u) (e c)", u=PLANES, e=2),
+            in_=Wv.rearrange("(g u p e) c -> p (g u) (e c)", g=PASSES, u=PLANES, e=2),
+        )
+        load(1)
 
         ident_bf = const.tile([P, P], BF16)
         make_identity(nc, ident_bf[:])
@@ -423,6 +426,7 @@ def tile_localselfattention_pa_t_kernel(tc, q, k_scaled, hidden_states, Wv, out)
             v_gather(0, h)
         v_quantise(0)
         v_share(0)
+        load(2)
 
         for i in range(-2, UNITS + 6):
             c, step = step_of(i)
@@ -468,6 +472,8 @@ def tile_localselfattention_pa_t_kernel(tc, q, k_scaled, hidden_states, Wv, out)
             if step_before == STEPS - 1:
                 v_quantise(c_before)
                 v_share(c_before)
+                if c_before + 2 < CHUNKS:
+                    load(c_before + 2)
 
             if step == K_STEP:
                 k_copy(c)

@@ -428,9 +428,12 @@ def tile_localselfattention_pa_t_kernel(tc, q, k_scaled, hidden_states, Wv, out)
         v_share(0)
         load(2)
 
-        for i in range(-2, UNITS + 6):
+        for i in range(-2, UNITS + 7):
             c, step = step_of(i)
             c_before, step_before = step_of(i - 1)
+
+            if exists(i - 6) and (i - 6) % BANK_UNITS == BANK_UNITS - 1:
+                divide_and_store((i - 6) // BANK_UNITS)
 
             if V_STEP <= step_before < STEPS:
                 v_gather(c_before, step_before - V_STEP)
@@ -458,17 +461,13 @@ def tile_localselfattention_pa_t_kernel(tc, q, k_scaled, hidden_states, Wv, out)
                 quantise_e(i - 3)
             if exists(i + 1):
                 move_own(i + 1)
-            if exists(i - 5) and (i - 5) % BANK_UNITS == BANK_UNITS - 1:
-                divide_and_store((i - 5) // BANK_UNITS)
 
             if V_STEP <= step < STEPS:
                 v_project(c, step - V_STEP)
-            if exists(i - 4) and not is_first(i - 4):
-                if is_second(i - 4):
-                    product(i - 5, i - 4)
-                product(i - 4, i - 4)
-            if exists(i - 4) and (i - 4) % BANK_UNITS == BANK_UNITS - 1:
-                invert_sums((i - 4) // BANK_UNITS)
+            if exists(i - 5):
+                product(i - 5, i - 4 if is_first(i - 5) else i - 5)
+            if exists(i - 5) and (i - 5) % BANK_UNITS == BANK_UNITS - 1:
+                invert_sums((i - 5) // BANK_UNITS)
             if step_before == STEPS - 1:
                 v_quantise(c_before)
                 v_share(c_before)

@@ -46,19 +46,19 @@ def tile_localselfattention_pa_t_kernel(tc, q, k_scaled, hidden_states, Wv, out)
 
     with ExitStack() as ctx:
         const = ctx.enter_context(tc.tile_pool(name="const", bufs=1))
-        loads = ctx.enter_context(tc.tile_pool(name="loads", bufs=2))
+        loads = ctx.enter_context(tc.tile_pool(name="loads", bufs=3))
         keep = ctx.enter_context(tc.tile_pool(name="keep", bufs=1))
-        work = ctx.enter_context(tc.tile_pool(name="work", bufs=3))
-        small = ctx.enter_context(tc.tile_pool(name="small", bufs=4))
-        codes = ctx.enter_context(tc.tile_pool(name="codes", bufs=4))
-        dots_psum = ctx.enter_context(tc.psum_pool(name="dots_psum", bufs=4))
+        work = ctx.enter_context(tc.tile_pool(name="work", bufs=5))
+        small = ctx.enter_context(tc.tile_pool(name="small", bufs=10))
+        codes = ctx.enter_context(tc.tile_pool(name="codes", bufs=9))
+        dots_psum = ctx.enter_context(tc.psum_pool(name="dots_psum", bufs=3))
         et_psum = ctx.enter_context(tc.psum_pool(name="et_psum", bufs=2))
         o_psum = ctx.enter_context(tc.psum_pool(name="o_psum", bufs=1))
-        prep_psum = ctx.enter_context(tc.psum_pool(name="prep_psum", bufs=1))
+        prep_psum = ctx.enter_context(tc.psum_pool(name="prep_psum", bufs=2))
 
         q_sb, k_sb, hs_sb = [], [], []
 
-        def load(n):
+        def load_qk(n):
             k_sb.append(loads.tile([P, H, TILES, D], BF16, name="k_sb"))
             q_sb.append(loads.tile([P, H, TILES, D], BF16, name="q_sb"))
             for rows, rows_sb in ((k_rows, k_sb[n]), (q_rows, q_sb[n])):
@@ -68,19 +68,23 @@ def tile_localselfattention_pa_t_kernel(tc, q, k_scaled, hidden_states, Wv, out)
                         out=rows_sb[:, h],
                         in_=rows[row : row + CHUNK, :].rearrange("(t p) d -> p t d", p=P),
                     )
+
+        def load_hs(n):
             hs_sb.append(loads.tile([P, TILES, HID], BF16, name="hs_sb"))
             nc.sync.dma_start(
                 out=hs_sb[n][:],
                 in_=hs_rows[n * CHUNK : (n + 1) * CHUNK, :].rearrange("(p t) k -> p t k", t=PACK),
             )
 
-        load(0)
+        load_qk(0)
+        load_qk(1)
+        load_hs(0)
         wv_raw = const.tile([P, PASSES, PACK, H * D], BF16)
         nc.sync.dma_start(
             out=wv_raw[:].rearrange("p g (u e) c -> p (g u) (e c)", u=PLANES, e=2),
             in_=Wv.rearrange("(g u p e) c -> p (g u) (e c)", g=PASSES, u=PLANES, e=2),
         )
-        load(1)
+        load_hs(1)
 
         ident_bf = const.tile([P, P], BF16)
         make_identity(nc, ident_bf[:])
@@ -142,22 +146,20 @@ def tile_localselfattention_pa_t_kernel(tc, q, k_scaled, hidden_states, Wv, out)
 
         live = {}
 
-        def prep_bank(c, shape, dtype):
-            if c == 0:
-                return dots_psum.tile(shape, dtype, tag="dots", name="prep_bank_0")
+        def prep_bank(shape, dtype):
             return prep_psum.tile(shape, dtype, tag="prep", name="prep_bank")
 
-        def qk_flip(c, rows_sb):
-            flipped = prep_bank(c, [P, H * TILES, P], BF16)
+        def qk_flip(c, which, rows_sb):
+            flipped = prep_bank([P, H * TILES, P], BF16)
             for h in range(H):
                 for t in range(TILES):
                     nc.tensor.transpose(flipped[:, h * TILES + t, :], rows_sb[:, h, t, :], ident_bf[:])
-            live["flipped"] = flipped
+            live[("flipped", c, which)] = flipped
 
         def q_copy(c):
             nc.scalar.copy(
                 out=qT[c][:].rearrange("p h s -> p (h s)").bitcast(F32),
-                in_=live["flipped"][:].rearrange("p a r -> p (a r)").bitcast(F32),
+                in_=live[("flipped", c, "q")][:].rearrange("p a r -> p (a r)").bitcast(F32),
             )
 
         def k_copy(c):
@@ -165,7 +167,7 @@ def tile_localselfattention_pa_t_kernel(tc, q, k_scaled, hidden_states, Wv, out)
                 out=kT[c][:].rearrange("p h s -> p (h s)").bitcast(F32).rearrange(
                     "p (a u x) -> p a u x", u=PLANES, x=RUN // 2
                 ),
-                in_=live["flipped"][:].rearrange("p a r -> p (a r)").bitcast(F32).rearrange(
+                in_=live[("flipped", c, "k")][:].rearrange("p a r -> p (a r)").bitcast(F32).rearrange(
                     "p (a x u) -> p a u x", u=PLANES, x=RUN // 2
                 ),
             )
@@ -180,28 +182,28 @@ def tile_localselfattention_pa_t_kernel(tc, q, k_scaled, hidden_states, Wv, out)
 
         def hs_flip(c, t):
             hs_words = hs_sb[c][:, t, :].bitcast(F32)
-            planes = prep_bank(c, [P, PASSES * PLANES, P], F32)
+            planes = prep_bank([P, PASSES * PLANES, P], F32)
             for b in range(PASSES * PLANES):
                 nc.tensor.transpose(planes[:, b, :], hs_words[:, b * P : (b + 1) * P], ident_f32[:])
-            live["hs_planes"] = planes
+            live[("hs_planes", c, t)] = planes
 
-        def hs_gather():
+        def hs_gather(c, t):
             hs_grp = work.tile([P, PASSES * CHUNK], BF16, align_bytes=64)
             nc.scalar.copy(
                 out=hs_grp[:].bitcast(F32).rearrange("p (g r u) -> p g r u", g=PASSES, u=PLANES),
-                in_=live["hs_planes"][:].rearrange("p (g u) r -> p g r u", u=PLANES),
+                in_=live[("hs_planes", c, t)][:].rearrange("p (g u) r -> p g r u", u=PLANES),
             )
-            live["hs_grp"] = hs_grp
+            live[("hs_grp", c, t)] = hs_grp
 
         def hs_quantise(c, t):
             nc.vector.quantize_mx(
                 out=hs_codes[c % 2][:, t].rearrange("p g r -> p (g r)").bitcast(FP8X4),
                 scales=hs_scales[c % 2][:, t].rearrange("p g r -> p (g r)"),
-                in_=live["hs_grp"][:],
+                in_=live[("hs_grp", c, t)][:],
             )
 
         def v_project(c, h):
-            v_ps = prep_bank(c, [P, TILES, D], F32)
+            v_ps = prep_bank([P, TILES, D], F32)
             for t in range(TILES):
                 for g in range(PASSES):
                     nc.tensor.matmul_mx(
@@ -213,10 +215,10 @@ def tile_localselfattention_pa_t_kernel(tc, q, k_scaled, hidden_states, Wv, out)
                         start=(g == 0),
                         stop=(g == PASSES - 1),
                     )
-            live["v_ps"] = v_ps
+            live[("v_ps", c, h)] = v_ps
 
         def v_gather(c, h):
-            nc.vector.tensor_copy(out=v_grp[c % 2][:, h], in_=live["v_ps"][:].rearrange("p t d -> p d t"))
+            nc.vector.tensor_copy(out=v_grp[c % 2][:, h], in_=live[("v_ps", c, h)][:].rearrange("p t d -> p d t"))
 
         def v_quantise(c):
             nc.vector.quantize_mx(
@@ -362,7 +364,10 @@ def tile_localselfattention_pa_t_kernel(tc, q, k_scaled, hidden_states, Wv, out)
             n, j, h = unit(u)
             bank = u // BANK_UNITS
             if u % BANK_UNITS == 0:
-                live[("o_ps", bank)] = o_psum.tile([P, BANK_UNITS, D], F32, tag="o", name="o_ps")
+                if n + 1 < CHUNKS:
+                    live[("o_ps", bank)] = o_psum.tile([P, BANK_UNITS, D], F32, tag="o", name="o_ps")
+                else:
+                    live[("o_ps", bank)] = prep_bank([P, BANK_UNITS, D], F32)
             factors = []
             if n > 0:
                 before = live[("e_pass", u, 2 if is_second(u) else 0)]
@@ -408,75 +413,80 @@ def tile_localselfattention_pa_t_kernel(tc, q, k_scaled, hidden_states, Wv, out)
         def exists(u):
             return 0 <= u < UNITS
 
-        def step_of(i):
-            if i < 0 or i // STEPS + 1 >= CHUNKS:
-                return None, STEPS
-            return i // STEPS + 1, i % STEPS
+        TABLE = (
+            (1, HS_STEP + 3), (1, K_STEP), (1, Q_STEP), (1, V_STEP),
+            (2, HS_STEP), (2, HS_STEP + 1), (2, HS_STEP + 2), (1, V_STEP + 1),
+        )
+        HEAD = {0: ((0, HS_STEP + 2), (0, HS_STEP + 3),), 1: ((0, V_STEP + 0),), 2: ((0, V_STEP + 1), (1, HS_STEP + 0),), 3: ((1, HS_STEP + 1),), 4: ((1, HS_STEP + 2),), 5: ((1, HS_STEP + 3),), 6: ((1, V_STEP + 0), (2, HS_STEP + 0),), 7: ((1, V_STEP + 1), (2, HS_STEP + 1),), 8: ((2, HS_STEP + 2),), -3: ((1, K_STEP),), -2: ((1, Q_STEP),), -1: ((0, HS_STEP + 0), (0, HS_STEP + 1),)}
 
-        qk_flip(0, k_sb[0])
-        k_copy(0)
-        qk_flip(0, q_sb[0])
-        q_copy(0)
-        for t in range(TILES):
-            hs_flip(0, t)
-            hs_gather()
-            hs_quantise(0, t)
-        for h in range(H):
-            v_project(0, h)
-            v_gather(0, h)
-        v_quantise(0)
-        v_share(0)
-        load(2)
+        def steps_of(i):
+            steps = list(HEAD.get(i, ()))
+            if i >= 8:
+                ahead, step = TABLE[i % STEPS]
+                if i // STEPS + ahead < CHUNKS:
+                    steps.append((i // STEPS + ahead, step))
+            return steps
 
-        for i in range(-2, UNITS + 7):
-            c, step = step_of(i)
-            c_before, step_before = step_of(i - 1)
-
-            if exists(i - 6) and (i - 6) % BANK_UNITS == BANK_UNITS - 1:
-                divide_and_store((i - 6) // BANK_UNITS)
-
-            if V_STEP <= step_before < STEPS:
-                v_gather(c_before, step_before - V_STEP)
-            if HS_STEP <= step_before < V_STEP:
-                hs_quantise(c_before, step_before - HS_STEP)
-
-            if exists(i - 1) and passes(i - 1):
-                flip_e(i - 1)
+        def do_flip(c, step):
             if step == K_STEP:
-                qk_flip(c, k_sb[c])
-            if step == Q_STEP:
-                qk_flip(c, q_sb[c])
-            if HS_STEP <= step < V_STEP:
+                qk_flip(c, "k", k_sb[c])
+            elif step == Q_STEP:
+                qk_flip(c, "q", q_sb[c])
+            elif step < V_STEP:
                 hs_flip(c, step - HS_STEP)
 
-            if exists(i):
-                exponentials(i)
-            if STEPS <= i + 1 < UNITS:
-                move_before(i + 1)
-            if exists(i + 2):
-                scores(i + 2)
-            if exists(i - 2) and passes(i - 2):
-                gather_e(i - 2)
-            if exists(i - 3) and passes(i - 3):
-                quantise_e(i - 3)
-            if exists(i + 1):
-                move_own(i + 1)
-
-            if V_STEP <= step < STEPS:
-                v_project(c, step - V_STEP)
-            if exists(i - 5):
-                product(i - 5, i - 4 if is_first(i - 5) else i - 5)
-            if exists(i - 5) and (i - 5) % BANK_UNITS == BANK_UNITS - 1:
-                invert_sums((i - 5) // BANK_UNITS)
-            if step_before == STEPS - 1:
-                v_quantise(c_before)
-                v_share(c_before)
-                if c_before + 2 < CHUNKS:
-                    load(c_before + 2)
-
+        def do_copy(c, step):
             if step == K_STEP:
                 k_copy(c)
-            if step == Q_STEP:
+            elif step == Q_STEP:
                 q_copy(c)
-            if HS_STEP <= step < V_STEP:
-                hs_gather()
+            elif step < V_STEP:
+                hs_gather(c, step - HS_STEP)
+
+        ctx.enter_context(tc.manual_schedule())
+        for step in (K_STEP, Q_STEP):
+            do_flip(0, step)
+            do_copy(0, step)
+
+        for i in range(-3, UNITS + 8 + 1):
+            if exists(i):
+                exponentials(i)
+            if exists(i - 2) and passes(i - 2):
+                gather_e(i - 2)
+            if STEPS <= i + 2 < UNITS:
+                move_before(i + 2)
+            if exists(i - 1) and passes(i - 1):
+                flip_e(i - 1)
+            for c, step in steps_of(i):
+                do_flip(c, step)
+            if exists(i + 3):
+                scores(i + 3)
+            if exists(i - 3) and passes(i - 3):
+                quantise_e(i - 3)
+            if exists(i + 2):
+                move_own(i + 2)
+            for c, step in steps_of(i - 1):
+                if step >= V_STEP:
+                    v_gather(c, step - V_STEP)
+            for c, step in steps_of(i - 1):
+                if HS_STEP <= step < V_STEP:
+                    hs_quantise(c, step - HS_STEP)
+            for c, step in steps_of(i - 2):
+                if step == STEPS - 1:
+                    v_quantise(c)
+                    v_share(c)
+            for c, step in steps_of(i):
+                if step == V_STEP and c + 2 < CHUNKS:
+                    load_qk(c + 2)
+                    load_hs(c + 2)
+            for c, step in steps_of(i):
+                if step >= V_STEP:
+                    v_project(c, step - V_STEP)
+            if exists(i - 8) and (i - 8) % BANK_UNITS == BANK_UNITS - 1:
+                divide_and_store((i - 8) // BANK_UNITS)
+            if exists(i - 7):
+                product(i - 7, i - 7 + (1 if is_first(i - 7) else 0))
+            if exists(i - 7) and (i - 7) % BANK_UNITS == BANK_UNITS - 1:
+                invert_sums((i - 7) // BANK_UNITS)
+            for c, step in steps_of(i):
+                do_copy(c, step)

@@ -61,8 +61,8 @@ def tile_localselfattention_pa_t_kernel(tc, q, k_scaled, hidden_states, Wv, out)
         def load_qk(n):
             k_sb.append(loads.tile([P, H, TILES, D], BF16, name="k_sb"))
             q_sb.append(loads.tile([P, H, TILES, D], BF16, name="q_sb"))
-            for rows, rows_sb in ((k_rows, k_sb[n]), (q_rows, q_sb[n])):
-                for h in range(H):
+            for h in range(H):
+                for rows, rows_sb in ((k_rows, k_sb[n]), (q_rows, q_sb[n])):
                     row = h * S + n * CHUNK
                     nc.sync.dma_start(
                         out=rows_sb[:, h],
@@ -112,15 +112,24 @@ def tile_localselfattention_pa_t_kernel(tc, q, k_scaled, hidden_states, Wv, out)
             for g, group in enumerate(GROUPS)
         ]
 
-        wv_grp = const.tile([P, PASSES, H * D, PACK], BF16, align_bytes=64)
-        nc.vector.tensor_copy(out=wv_grp[:], in_=wv_raw[:].rearrange("p g t c -> p g c t"))
         wv_codes = const.tile([P, PASSES, H * D], U32, align_bytes=64)
         wv_scales = const.tile([P, PASSES, H * D], U8, align_bytes=64)
-        nc.vector.quantize_mx(
-            out=wv_codes[:].rearrange("p g c -> p (g c)").bitcast(FP8X4),
-            scales=wv_scales[:].rearrange("p g c -> p (g c)"),
-            in_=wv_grp[:].rearrange("p g c t -> p (g c t)"),
-        )
+
+        def wv_quantise():
+            wv_grp = const.tile([P, PASSES, H * D, PACK], BF16, align_bytes=64)
+            nc.gpsimd.tensor_scalar(
+                out=wv_grp[:],
+                in0=wv_raw[:].rearrange("p g t c -> p g c t"),
+                scalar1=1.0,
+                scalar2=0.0,
+                op0=ALU.mult,
+                op1=ALU.add,
+            )
+            nc.vector.quantize_mx(
+                out=wv_codes[:].rearrange("p g c -> p (g c)").bitcast(FP8X4),
+                scales=wv_scales[:].rearrange("p g c -> p (g c)"),
+                in_=wv_grp[:].rearrange("p g c t -> p (g c t)"),
+            )
 
         qT = [keep.tile([P, H, CHUNK], BF16, name="qT_%d" % n) for n in range(CHUNKS)]
         kT = [keep.tile([P, H, CHUNK], BF16, name="kT_%d" % n) for n in range(CHUNKS)]
@@ -149,25 +158,27 @@ def tile_localselfattention_pa_t_kernel(tc, q, k_scaled, hidden_states, Wv, out)
         def prep_bank(shape, dtype):
             return prep_psum.tile(shape, dtype, tag="prep", name="prep_bank")
 
-        def qk_flip(c, which, rows_sb):
-            flipped = prep_bank([P, H * TILES, P], BF16)
-            for h in range(H):
+        def qk_flip(c, which, rows_sb, heads):
+            flipped = prep_bank([P, len(heads), CHUNK], BF16)
+            for at, h in enumerate(heads):
                 for t in range(TILES):
-                    nc.tensor.transpose(flipped[:, h * TILES + t, :], rows_sb[:, h, t, :], ident_bf[:])
-            live[("flipped", c, which)] = flipped
+                    nc.tensor.transpose(
+                        flipped[:, at, t * P : (t + 1) * P], rows_sb[:, h, t, :], ident_bf[:]
+                    )
+            live[("flipped", c, which, heads)] = flipped
 
-        def q_copy(c):
-            nc.scalar.copy(
-                out=qT[c][:].rearrange("p h s -> p (h s)").bitcast(F32),
-                in_=live[("flipped", c, "q")][:].rearrange("p a r -> p (a r)").bitcast(F32),
+        def q_copy(c, heads, copy):
+            copy(
+                out=qT[c][:, heads.start : heads.stop].rearrange("p h s -> p (h s)").bitcast(F32),
+                in_=live[("flipped", c, "q", heads)][:].rearrange("p h s -> p (h s)").bitcast(F32),
             )
 
-        def k_copy(c):
-            nc.scalar.copy(
-                out=kT[c][:].rearrange("p h s -> p (h s)").bitcast(F32).rearrange(
+        def k_copy(c, heads, copy):
+            copy(
+                out=kT[c][:, heads.start : heads.stop].rearrange("p h s -> p (h s)").bitcast(F32).rearrange(
                     "p (a u x) -> p a u x", u=PLANES, x=RUN // 2
                 ),
-                in_=live[("flipped", c, "k")][:].rearrange("p a r -> p (a r)").bitcast(F32).rearrange(
+                in_=live[("flipped", c, "k", heads)][:].rearrange("p h s -> p (h s)").bitcast(F32).rearrange(
                     "p (a x u) -> p a u x", u=PLANES, x=RUN // 2
                 ),
             )
@@ -417,11 +428,11 @@ def tile_localselfattention_pa_t_kernel(tc, q, k_scaled, hidden_states, Wv, out)
             (1, HS_STEP + 3), (1, K_STEP), (1, Q_STEP), (1, V_STEP),
             (2, HS_STEP), (2, HS_STEP + 1), (2, HS_STEP + 2), (1, V_STEP + 1),
         )
-        HEAD = {0: ((0, HS_STEP + 2), (0, HS_STEP + 3),), 1: ((0, V_STEP + 0),), 2: ((0, V_STEP + 1), (1, HS_STEP + 0),), 3: ((1, HS_STEP + 1),), 4: ((1, HS_STEP + 2),), 5: ((1, HS_STEP + 3),), 6: ((1, V_STEP + 0), (2, HS_STEP + 0),), 7: ((1, V_STEP + 1), (2, HS_STEP + 1),), 8: ((2, HS_STEP + 2),), -3: ((1, K_STEP),), -2: ((1, Q_STEP),), -1: ((0, HS_STEP + 0), (0, HS_STEP + 1),)}
+        HEAD = {0: ((0, HS_STEP + 0),), 1: ((0, HS_STEP + 1),), 2: ((0, HS_STEP + 2),), 3: ((0, HS_STEP + 3),), 4: ((0, V_STEP + 0), (1, HS_STEP + 0),), 5: ((0, V_STEP + 1), (1, HS_STEP + 1),), 6: ((1, HS_STEP + 2),), 7: ((1, HS_STEP + 3),), 8: ((1, V_STEP + 0), (2, HS_STEP + 0),), 9: ((1, V_STEP + 1), (2, K_STEP),), 10: ((2, Q_STEP), (2, HS_STEP + 1),), 11: ((2, HS_STEP + 2),), 12: ((2, HS_STEP + 3),), 13: ((2, V_STEP + 0), (3, HS_STEP + 0),), 14: ((2, V_STEP + 1), (3, HS_STEP + 1),), 15: ((3, HS_STEP + 2),), -3: ((1, K_STEP),), -2: ((1, Q_STEP),)}
 
         def steps_of(i):
             steps = list(HEAD.get(i, ()))
-            if i >= 8:
+            if i >= 16:
                 ahead, step = TABLE[i % STEPS]
                 if i // STEPS + ahead < CHUNKS:
                     steps.append((i // STEPS + ahead, step))
@@ -429,26 +440,21 @@ def tile_localselfattention_pa_t_kernel(tc, q, k_scaled, hidden_states, Wv, out)
 
         def do_flip(c, step):
             if step == K_STEP:
-                qk_flip(c, "k", k_sb[c])
+                qk_flip(c, "k", k_sb[c], range(H))
             elif step == Q_STEP:
-                qk_flip(c, "q", q_sb[c])
+                qk_flip(c, "q", q_sb[c], range(H))
             elif step < V_STEP:
                 hs_flip(c, step - HS_STEP)
 
         def do_copy(c, step):
             if step == K_STEP:
-                k_copy(c)
+                k_copy(c, range(H), nc.scalar.copy)
             elif step == Q_STEP:
-                q_copy(c)
+                q_copy(c, range(H), nc.vector.tensor_copy if c < 2 else nc.scalar.copy)
             elif step < V_STEP:
                 hs_gather(c, step - HS_STEP)
 
-        ctx.enter_context(tc.manual_schedule())
-        for step in (K_STEP, Q_STEP):
-            do_flip(0, step)
-            do_copy(0, step)
-
-        for i in range(-3, UNITS + 8 + 1):
+        def tick(i):
             if exists(i):
                 exponentials(i)
             if exists(i - 2) and passes(i - 2):
@@ -463,6 +469,8 @@ def tile_localselfattention_pa_t_kernel(tc, q, k_scaled, hidden_states, Wv, out)
                 scores(i + 3)
             if exists(i - 3) and passes(i - 3):
                 quantise_e(i - 3)
+            if exists(i - 10) and (i - 10) % BANK_UNITS == BANK_UNITS - 1:
+                divide_and_store((i - 10) // BANK_UNITS)
             if exists(i + 2):
                 move_own(i + 2)
             for c, step in steps_of(i - 1):
@@ -479,14 +487,26 @@ def tile_localselfattention_pa_t_kernel(tc, q, k_scaled, hidden_states, Wv, out)
                 if step == V_STEP and c + 2 < CHUNKS:
                     load_qk(c + 2)
                     load_hs(c + 2)
+            if i == 2:
+                wv_quantise()
             for c, step in steps_of(i):
                 if step >= V_STEP:
                     v_project(c, step - V_STEP)
-            if exists(i - 8) and (i - 8) % BANK_UNITS == BANK_UNITS - 1:
-                divide_and_store((i - 8) // BANK_UNITS)
-            if exists(i - 7):
-                product(i - 7, i - 7 + (1 if is_first(i - 7) else 0))
-            if exists(i - 7) and (i - 7) % BANK_UNITS == BANK_UNITS - 1:
-                invert_sums((i - 7) // BANK_UNITS)
+            if exists(i - 9):
+                product(i - 9, i - 9 + (1 if is_first(i - 9) else 0))
+            if exists(i - 9) and (i - 9) % BANK_UNITS == BANK_UNITS - 1:
+                invert_sums((i - 9) // BANK_UNITS)
             for c, step in steps_of(i):
                 do_copy(c, step)
+
+        HEAD_TICKS = 4
+        with tc.manual_schedule():
+            for h in range(H):
+                qk_flip(0, "k", k_sb[0], range(h, h + 1))
+                k_copy(0, range(h, h + 1), nc.scalar.copy)
+                qk_flip(0, "q", q_sb[0], range(h, h + 1))
+                q_copy(0, range(h, h + 1), nc.vector.tensor_copy)
+            for i in range(-3, HEAD_TICKS):
+                tick(i)
+        for i in range(HEAD_TICKS, UNITS + 10 + 1):
+            tick(i)

@@ -29,6 +29,7 @@ QUADRANT = P // QUARTERS
 RUN = P // PLANES
 GROUPS = (((0, 0), (2, 0)), ((0, 1), (2, 1)), ((1, 0), (1, 1)), ((3, 0),), ((3, 1),))
 ORDER = [(g, place) for g in range(len(GROUPS)) for place in range(len(GROUPS[g]))]
+LAST = UNITS - 1
 BANK_UNITS = 4
 STEPS = TILES * H
 V_WORDS = H * D
@@ -48,7 +49,7 @@ def tile_localselfattention_pa_t_kernel(tc, q, k_scaled, hidden_states, Wv, out)
         const = ctx.enter_context(tc.tile_pool(name="const", bufs=1))
         loads = ctx.enter_context(tc.tile_pool(name="loads", bufs=3))
         keep = ctx.enter_context(tc.tile_pool(name="keep", bufs=1))
-        work = ctx.enter_context(tc.tile_pool(name="work", bufs=5))
+        work = ctx.enter_context(tc.tile_pool(name="work", bufs=6))
         small = ctx.enter_context(tc.tile_pool(name="small", bufs=10))
         codes = ctx.enter_context(tc.tile_pool(name="codes", bufs=9))
         dots_psum = ctx.enter_context(tc.psum_pool(name="dots_psum", bufs=3))
@@ -85,6 +86,8 @@ def tile_localselfattention_pa_t_kernel(tc, q, k_scaled, hidden_states, Wv, out)
             in_=Wv.rearrange("(g u p e) c -> p (g u) (e c)", g=PASSES, u=PLANES, e=2),
         )
         load_hs(1)
+        load_qk(2)
+        load_hs(2)
 
         ident_bf = const.tile([P, P], BF16)
         make_identity(nc, ident_bf[:])
@@ -277,6 +280,16 @@ def tile_localselfattention_pa_t_kernel(tc, q, k_scaled, hidden_states, Wv, out)
                 return range(1, 3 if n > 0 else 2)
             return range(0 if n > 0 else 1, 2)
 
+        def parts(u):
+            if u == LAST:
+                return [slice(0, QUARTERS), slice(QUARTERS, 2 * QUARTERS)]
+            return [slots(u)]
+
+        def runs(u):
+            if u == LAST:
+                return [range(s, s + 1) for s in passes(u)]
+            return [passes(u)]
+
         def scores(u):
             n, j, h = unit(u)
             q_cols = qT[n][:, h, j * P : (j + 1) * P]
@@ -329,43 +342,60 @@ def tile_localselfattention_pa_t_kernel(tc, q, k_scaled, hidden_states, Wv, out)
             bank, at = u // BANK_UNITS, column(u)
             if u % BANK_UNITS == 0:
                 live[("sums", bank)] = small.tile([P, BANK_UNITS], F32, name="sums")
-            nc.scalar.activation(
-                out=e_sb[ORDER[u % STEPS][0]][:, :, slots(u), :].rearrange("p u s x -> p s u x"),
-                in_=live[("minus_dots", u)].rearrange("p (s u x) -> p s u x", u=PLANES, x=RUN),
-                func=EXP,
-                bias=live[("lows", u)][:, 1:2],
-                scale=-1.0,
-                accum_out=live[("sums", bank)][:, at : at + 1],
-            )
+            if u == LAST:
+                live["last_sum"] = small.tile([P, 1], F32, name="last_sum")
+            for part in parts(u):
+                columns = slice((part.start - slots(u).start) * P, (part.stop - slots(u).start) * P)
+                nc.scalar.activation(
+                    out=e_sb[ORDER[u % STEPS][0]][:, :, part, :].rearrange("p u s x -> p s u x"),
+                    in_=live[("minus_dots", u)][:, columns].rearrange("p (s u x) -> p s u x", u=PLANES, x=RUN),
+                    func=EXP,
+                    bias=live[("lows", u)][:, 1:2],
+                    scale=-1.0,
+                    accum_out=(
+                        live[("sums", bank)][:, at : at + 1]
+                        if part.start == slots(u).start
+                        else live["last_sum"][:]
+                    ),
+                )
 
         def flip_e(u):
             e_words = e_sb[ORDER[u % STEPS][0]][:].rearrange("p u s x -> p u (s x)").bitcast(F32)
-            eT = et_psum.tile([P, 2, PLANES, P], F32, tag="eT")
-            for w, s in enumerate(passes(u)):
-                for b in range(PLANES):
-                    nc.tensor.transpose(eT[:, w, b, :], e_words[:, b, s * P : (s + 1) * P], ident_f32[:])
-            live[("eT", u)] = eT
+            for run in runs(u):
+                eT = et_psum.tile([P, 2, PLANES, P], F32, tag="eT")
+                for w, s in enumerate(run):
+                    for b in range(PLANES):
+                        nc.tensor.transpose(eT[:, w, b, :], e_words[:, b, s * P : (s + 1) * P], ident_f32[:])
+                live[("eT", u, run)] = eT
 
         def gather_e(u):
-            count = len(passes(u))
-            e_grp = work.tile([P, 2 * CHUNK], BF16, align_bytes=64)
-            nc.scalar.copy(
-                out=e_grp[:, : count * CHUNK].bitcast(F32).rearrange("p (w r u) -> p w r u", w=count, u=PLANES),
-                in_=live[("eT", u)][:, :count].rearrange("p w u r -> p w r u"),
-            )
-            live[("e_grp", u)] = e_grp
+            copy = nc.vector.tensor_copy if UNITS - 3 <= u < LAST else nc.scalar.copy
+            for run in runs(u):
+                count = len(run)
+                e_grp = work.tile([P, 2 * CHUNK], BF16, align_bytes=64)
+                copy(
+                    out=e_grp[:, : count * CHUNK].bitcast(F32).rearrange(
+                        "p (w r u) -> p w r u", w=count, u=PLANES
+                    ),
+                    in_=live[("eT", u, run)][:, :count].rearrange("p w u r -> p w r u"),
+                )
+                live[("e_grp", u, run)] = e_grp
 
         def quantise_e(u):
-            count = len(passes(u))
-            e_codes = codes.tile([P, 2 * P], U32, align_bytes=64)
-            e_scales = codes.tile([P, 2 * P], U8, align_bytes=64)
-            nc.vector.quantize_mx(
-                out=e_codes[:, : count * P].bitcast(FP8X4),
-                scales=e_scales[:, : count * P],
-                in_=live[("e_grp", u)][:, : count * CHUNK],
-            )
-            for w, s in enumerate(passes(u)):
-                live[("e_pass", u, s)] = (e_codes[:, w * P : (w + 1) * P], e_scales[:, w * P : (w + 1) * P])
+            for run in runs(u):
+                count = len(run)
+                e_codes = codes.tile([P, 2 * P], U32, align_bytes=64)
+                e_scales = codes.tile([P, 2 * P], U8, align_bytes=64)
+                nc.vector.quantize_mx(
+                    out=e_codes[:, : count * P].bitcast(FP8X4),
+                    scales=e_scales[:, : count * P],
+                    in_=live[("e_grp", u, run)][:, : count * CHUNK],
+                )
+                for w, s in enumerate(run):
+                    live[("e_pass", u, s)] = (
+                        e_codes[:, w * P : (w + 1) * P],
+                        e_scales[:, w * P : (w + 1) * P],
+                    )
 
         def column(u):
             n, j, h = unit(u)
@@ -379,6 +409,10 @@ def tile_localselfattention_pa_t_kernel(tc, q, k_scaled, hidden_states, Wv, out)
                     live[("o_ps", bank)] = o_psum.tile([P, BANK_UNITS, D], F32, tag="o", name="o_ps")
                 else:
                     live[("o_ps", bank)] = prep_bank([P, BANK_UNITS, D], F32)
+            o_ps, at = live[("o_ps", bank)], column(u)
+            if u == LAST:
+                live["last_o_ps"] = o_psum.tile([P, BANK_UNITS, D], F32, tag="o", name="o_ps")
+                o_ps = live["last_o_ps"]
             factors = []
             if n > 0:
                 before = live[("e_pass", u, 2 if is_second(u) else 0)]
@@ -393,7 +427,7 @@ def tile_localselfattention_pa_t_kernel(tc, q, k_scaled, hidden_states, Wv, out)
             factors.append((live[("e_pass", last, 1)], v_own))
             for w, (e_side, v_side) in enumerate(factors):
                 nc.tensor.matmul_mx(
-                    out=live[("o_ps", bank)][:, column(u), :],
+                    out=o_ps[:, at, :],
                     lhsT=e_side[0].bitcast(FP8X4),
                     lhsT_scale=e_side[1],
                     rhs=v_side[0],
@@ -402,22 +436,39 @@ def tile_localselfattention_pa_t_kernel(tc, q, k_scaled, hidden_states, Wv, out)
                     stop=(w == len(factors) - 1),
                 )
 
-        def invert_sums(bank):
+        def invert_sums(bank, columns):
+            if columns.stop == BANK_UNITS and bank == LAST // BANK_UNITS:
+                last = live[("sums", bank)][:, BANK_UNITS - 1 :]
+                nc.vector.tensor_tensor(out=last, in0=last, in1=live["last_sum"][:], op=ALU.add)
             inverse = small.tile([P, BANK_UNITS], F32)
-            nc.vector.reciprocal(out=inverse[:], in_=live[("sums", bank)][:])
+            nc.vector.reciprocal(out=inverse[:, columns], in_=live[("sums", bank)][:, columns])
             live[("inverse", bank)] = inverse
 
-        def divide_and_store(bank):
+        def divide_and_store(bank, columns):
+            count = columns.stop - columns.start
             o_sb = work.tile([P, BANK_UNITS, D], F32)
             nc.vector.tensor_tensor(
-                out=o_sb[:],
-                in0=live[("o_ps", bank)][:],
-                in1=live[("inverse", bank)][:].unsqueeze(2).to_broadcast([P, BANK_UNITS, D]),
+                out=o_sb[:, columns],
+                in0=(live["last_o_ps"] if columns == finished(LAST) else live[("o_ps", bank)])[:, columns],
+                in1=live[("inverse", bank)][:, columns].unsqueeze(2).to_broadcast([P, count, D]),
                 op=ALU.mult,
             )
             n, x = bank // 2, bank % 2
-            rows = out_rows[n * CHUNK : (n + 1) * CHUNK, :].rearrange("(a x p) c -> x p a c", a=2, x=2)
-            nc.sync.dma_start(out=rows[x], in_=o_sb[:].rearrange("p (a h) d -> p a (h d)", a=2))
+            rows = out_rows[n * CHUNK : (n + 1) * CHUNK, :].rearrange("(a x p) c -> x p a c", a=2, x=2)[x]
+            if count == BANK_UNITS:
+                nc.sync.dma_start(out=rows, in_=o_sb[:].rearrange("p (a h) d -> p a (h d)", a=2))
+            else:
+                for at in range(columns.start, columns.stop):
+                    nc.sync.dma_start(
+                        out=rows[:, at // H, at % H * D : (at % H + 1) * D], in_=o_sb[:, at, :]
+                    )
+
+        def finished(u):
+            if u == LAST:
+                return slice(BANK_UNITS - 1, BANK_UNITS)
+            if u == LAST - 1:
+                return slice(0, BANK_UNITS - 1)
+            return slice(0, BANK_UNITS) if u % BANK_UNITS == BANK_UNITS - 1 else None
 
         K_STEP, Q_STEP, HS_STEP, V_STEP = 0, 1, 2, 2 + TILES
 
@@ -428,15 +479,22 @@ def tile_localselfattention_pa_t_kernel(tc, q, k_scaled, hidden_states, Wv, out)
             (1, HS_STEP + 3), (1, K_STEP), (1, Q_STEP), (1, V_STEP),
             (2, HS_STEP), (2, HS_STEP + 1), (2, HS_STEP + 2), (1, V_STEP + 1),
         )
-        HEAD = {0: ((0, HS_STEP + 0),), 1: ((0, HS_STEP + 1),), 2: ((0, HS_STEP + 2),), 3: ((0, HS_STEP + 3),), 4: ((0, V_STEP + 0), (1, HS_STEP + 0),), 5: ((0, V_STEP + 1), (1, HS_STEP + 1),), 6: ((1, HS_STEP + 2),), 7: ((1, HS_STEP + 3),), 8: ((1, V_STEP + 0), (2, HS_STEP + 0),), 9: ((1, V_STEP + 1), (2, K_STEP),), 10: ((2, Q_STEP), (2, HS_STEP + 1),), 11: ((2, HS_STEP + 2),), 12: ((2, HS_STEP + 3),), 13: ((2, V_STEP + 0), (3, HS_STEP + 0),), 14: ((2, V_STEP + 1), (3, HS_STEP + 1),), 15: ((3, HS_STEP + 2),), -3: ((1, K_STEP),), -2: ((1, Q_STEP),)}
+        HEAD = {1: ((0, HS_STEP + 0),), 2: ((0, HS_STEP + 1),), 3: ((0, HS_STEP + 2),), 4: ((0, HS_STEP + 3),), 5: ((0, V_STEP + 0), (1, HS_STEP + 0),), 6: ((0, V_STEP + 1), (1, HS_STEP + 1),), 7: ((1, HS_STEP + 2),), 8: ((1, HS_STEP + 3),), 9: ((1, V_STEP + 0), (2, K_STEP),), 10: ((1, V_STEP + 1), (2, Q_STEP),), 11: ((2, HS_STEP + 0),), 12: ((2, HS_STEP + 1),), 13: ((2, HS_STEP + 2),), 14: ((2, HS_STEP + 3),), 15: ((2, V_STEP + 0), (3, K_STEP),), 16: ((2, V_STEP + 1), (3, Q_STEP),), 17: ((3, HS_STEP + 0),), 18: ((3, HS_STEP + 1),), 19: ((3, HS_STEP + 2),), 20: ((3, HS_STEP + 3),), 21: ((3, V_STEP + 0), (4, HS_STEP + 0),), 22: ((4, HS_STEP + 1),), 23: ((3, V_STEP + 1), (4, HS_STEP + 2),), -3: ((1, K_STEP),), -2: ((1, Q_STEP),)}
 
         def steps_of(i):
             steps = list(HEAD.get(i, ()))
-            if i >= 16:
+            if i >= 24:
                 ahead, step = TABLE[i % STEPS]
                 if i // STEPS + ahead < CHUNKS:
                     steps.append((i // STEPS + ahead, step))
             return steps
+
+        def warm_up():
+            zeros = const.tile([P, CHUNK], BF16)
+            nc.vector.memset(zeros[:], 0.0)
+            idle = dots_psum.tile([P, CHUNK], F32, tag="dots", name="idle")
+            for repeat in range(5):
+                nc.tensor.matmul(out=idle[:], lhsT=zeros[:, :P], rhs=zeros[:], start=True, stop=True)
 
         def do_flip(c, step):
             if step == K_STEP:
@@ -459,20 +517,20 @@ def tile_localselfattention_pa_t_kernel(tc, q, k_scaled, hidden_states, Wv, out)
                 exponentials(i)
             if exists(i - 2) and passes(i - 2):
                 gather_e(i - 2)
-            if STEPS <= i + 2 < UNITS:
-                move_before(i + 2)
+            if STEPS <= i + 3 < UNITS:
+                move_before(i + 3)
             if exists(i - 1) and passes(i - 1):
                 flip_e(i - 1)
             for c, step in steps_of(i):
                 do_flip(c, step)
-            if exists(i + 3):
-                scores(i + 3)
+            if exists(i + 4):
+                scores(i + 4)
             if exists(i - 3) and passes(i - 3):
                 quantise_e(i - 3)
-            if exists(i - 10) and (i - 10) % BANK_UNITS == BANK_UNITS - 1:
-                divide_and_store((i - 10) // BANK_UNITS)
-            if exists(i + 2):
-                move_own(i + 2)
+            if exists(i - 10) and finished(i - 10):
+                divide_and_store((i - 10) // BANK_UNITS, finished(i - 10))
+            if exists(i + 3):
+                move_own(i + 3)
             for c, step in steps_of(i - 1):
                 if step >= V_STEP:
                     v_gather(c, step - V_STEP)
@@ -483,30 +541,30 @@ def tile_localselfattention_pa_t_kernel(tc, q, k_scaled, hidden_states, Wv, out)
                 if step == STEPS - 1:
                     v_quantise(c)
                     v_share(c)
-            for c, step in steps_of(i):
-                if step == V_STEP and c + 2 < CHUNKS:
-                    load_qk(c + 2)
-                    load_hs(c + 2)
-            if i == 2:
+            if i >= 0 and i % STEPS == STEPS // 2 and i // STEPS + 3 < CHUNKS:
+                load_qk(i // STEPS + 3)
+                load_hs(i // STEPS + 3)
+            if i == 3:
                 wv_quantise()
             for c, step in steps_of(i):
                 if step >= V_STEP:
                     v_project(c, step - V_STEP)
             if exists(i - 9):
                 product(i - 9, i - 9 + (1 if is_first(i - 9) else 0))
-            if exists(i - 9) and (i - 9) % BANK_UNITS == BANK_UNITS - 1:
-                invert_sums((i - 9) // BANK_UNITS)
+            if exists(i - 9) and finished(i - 9):
+                invert_sums((i - 9) // BANK_UNITS, finished(i - 9))
             for c, step in steps_of(i):
                 do_copy(c, step)
 
         HEAD_TICKS = 4
         with tc.manual_schedule():
+            warm_up()
             for h in range(H):
                 qk_flip(0, "k", k_sb[0], range(h, h + 1))
                 k_copy(0, range(h, h + 1), nc.scalar.copy)
                 qk_flip(0, "q", q_sb[0], range(h, h + 1))
                 q_copy(0, range(h, h + 1), nc.vector.tensor_copy)
-            for i in range(-3, HEAD_TICKS):
+            for i in range(-4, HEAD_TICKS):
                 tick(i)
         for i in range(HEAD_TICKS, UNITS + 10 + 1):
             tick(i)

@@ -232,7 +232,8 @@ def tile_localselfattention_pa_t_kernel(tc, q, k_scaled, hidden_states, Wv, out)
             live[("v_ps", c, h)] = v_ps
 
         def v_gather(c, h):
-            nc.vector.tensor_copy(out=v_grp[c % 2][:, h], in_=live[("v_ps", c, h)][:].rearrange("p t d -> p d t"))
+            copy = nc.vector.tensor_copy if h == 0 else nc.scalar.copy
+            copy(out=v_grp[c % 2][:, h], in_=live[("v_ps", c, h)][:].rearrange("p t d -> p d t"))
 
         def v_quantise(c):
             nc.vector.quantize_mx(
@@ -369,7 +370,7 @@ def tile_localselfattention_pa_t_kernel(tc, q, k_scaled, hidden_states, Wv, out)
                 live[("eT", u, run)] = eT
 
         def gather_e(u):
-            copy = nc.vector.tensor_copy if UNITS - 3 <= u < LAST else nc.scalar.copy
+            copy = nc.vector.tensor_copy if UNITS - 2 <= u < LAST else nc.scalar.copy
             for run in runs(u):
                 count = len(run)
                 e_grp = work.tile([P, 2 * CHUNK], BF16, align_bytes=64)
@@ -489,11 +490,12 @@ def tile_localselfattention_pa_t_kernel(tc, q, k_scaled, hidden_states, Wv, out)
                     steps.append((i // STEPS + ahead, step))
             return steps
 
-        def warm_up():
-            zeros = const.tile([P, CHUNK], BF16)
-            nc.vector.memset(zeros[:], 0.0)
+        zeros = const.tile([P, CHUNK], BF16)
+        nc.vector.memset(zeros[:], 0.0)
+
+        def warm_up(count):
             idle = dots_psum.tile([P, CHUNK], F32, tag="dots", name="idle")
-            for repeat in range(5):
+            for repeat in range(count):
                 nc.tensor.matmul(out=idle[:], lhsT=zeros[:, :P], rhs=zeros[:], start=True, stop=True)
 
         def do_flip(c, step):
@@ -525,6 +527,8 @@ def tile_localselfattention_pa_t_kernel(tc, q, k_scaled, hidden_states, Wv, out)
                 do_flip(c, step)
             if exists(i + 4):
                 scores(i + 4)
+            elif 0 < i < UNITS:
+                warm_up(2)
             if exists(i - 3) and passes(i - 3):
                 quantise_e(i - 3)
             if exists(i - 10) and finished(i - 10):
@@ -558,7 +562,7 @@ def tile_localselfattention_pa_t_kernel(tc, q, k_scaled, hidden_states, Wv, out)
 
         HEAD_TICKS = 4
         with tc.manual_schedule():
-            warm_up()
+            warm_up(5)
             for h in range(H):
                 qk_flip(0, "k", k_sb[0], range(h, h + 1))
                 k_copy(0, range(h, h + 1), nc.scalar.copy)

@@ -49,7 +49,7 @@ def tile_localselfattention_pa_t_kernel(tc, q, k_scaled, hidden_states, Wv, out)
         const = ctx.enter_context(tc.tile_pool(name="const", bufs=1))
         loads = ctx.enter_context(tc.tile_pool(name="loads", bufs=3))
         keep = ctx.enter_context(tc.tile_pool(name="keep", bufs=1))
-        work = ctx.enter_context(tc.tile_pool(name="work", bufs=6))
+        work = ctx.enter_context(tc.tile_pool(name="work", bufs=8))
         small = ctx.enter_context(tc.tile_pool(name="small", bufs=10))
         codes = ctx.enter_context(tc.tile_pool(name="codes", bufs=9))
         dots_psum = ctx.enter_context(tc.psum_pool(name="dots_psum", bufs=3))
@@ -519,22 +519,22 @@ def tile_localselfattention_pa_t_kernel(tc, q, k_scaled, hidden_states, Wv, out)
                 exponentials(i)
             if exists(i - 2) and passes(i - 2):
                 gather_e(i - 2)
-            if STEPS <= i + 3 < UNITS:
-                move_before(i + 3)
+            if STEPS <= i + 4 < UNITS:
+                move_before(i + 4)
             if exists(i - 1) and passes(i - 1):
                 flip_e(i - 1)
             for c, step in steps_of(i):
                 do_flip(c, step)
-            if exists(i + 4):
-                scores(i + 4)
+            if exists(i + 5):
+                scores(i + 5)
             elif 0 < i < UNITS:
                 warm_up(2)
             if exists(i - 3) and passes(i - 3):
                 quantise_e(i - 3)
             if exists(i - 10) and finished(i - 10):
                 divide_and_store((i - 10) // BANK_UNITS, finished(i - 10))
-            if exists(i + 3):
-                move_own(i + 3)
+            if exists(i + 4):
+                move_own(i + 4)
             for c, step in steps_of(i - 1):
                 if step >= V_STEP:
                     v_gather(c, step - V_STEP)
@@ -568,7 +568,7 @@ def tile_localselfattention_pa_t_kernel(tc, q, k_scaled, hidden_states, Wv, out)
                 k_copy(0, range(h, h + 1), nc.scalar.copy)
                 qk_flip(0, "q", q_sb[0], range(h, h + 1))
                 q_copy(0, range(h, h + 1), nc.vector.tensor_copy)
-            for i in range(-4, HEAD_TICKS):
+            for i in range(-5, HEAD_TICKS):
                 tick(i)
         for i in range(HEAD_TICKS, UNITS + 10 + 1):
             tick(i)

from contextlib import ExitStack

import concourse.mybir as mybir
from concourse.masks import make_identity

BF16 = mybir.dt.bfloat16
F32 = mybir.dt.float32
U32 = mybir.dt.uint32
U8 = mybir.dt.uint8
I32 = mybir.dt.int32
FP8X4 = mybir.dt.float8_e4m3fn_x4
ALU = mybir.AluOpType
EXP = mybir.ActivationFunctionType.Exp

P = 128
S = 4096
HID = 1024
H = 2
D = 128
CHUNK = 512
CHUNKS = S // CHUNK
TILES = CHUNK // P
PASSES = HID // CHUNK
PLANES = 2
PACK = 4
UNITS = CHUNKS * TILES * H
QUARTERS = 4
QUADRANT = P // QUARTERS
RUN = P // PLANES
GROUPS = (((0, 0), (2, 0)), ((0, 1), (2, 1)), ((1, 0), (1, 1)), ((3, 0),), ((3, 1),))
ORDER = [(g, place) for g in range(len(GROUPS)) for place in range(len(GROUPS[g]))]
LAST = UNITS - 1
BANK_UNITS = 4
STEPS = TILES * H
V_WORDS = H * D
MASK_VALUE = -1e9

FLOPS = 2 * S * HID * H * D + 2 * 2 * H * D * ((CHUNKS - 1) * CHUNK * 2 * CHUNK + CHUNK * CHUNK)


def tile_localselfattention_pa_t_kernel(tc, q, k_scaled, hidden_states, Wv, out):
    nc = tc.nc
    q_rows = q.flatten_outer_dims()
    k_rows = k_scaled.flatten_outer_dims()
    hs_rows = hidden_states.flatten_outer_dims()
    out_rows = out.flatten_outer_dims()

    with ExitStack() as ctx:
        const = ctx.enter_context(tc.tile_pool(name="const", bufs=1))
        loads = ctx.enter_context(tc.tile_pool(name="loads", bufs=3))
        keep = ctx.enter_context(tc.tile_pool(name="keep", bufs=1))
        work = ctx.enter_context(tc.tile_pool(name="work", bufs=8))
        small = ctx.enter_context(tc.tile_pool(name="small", bufs=10))
        codes = ctx.enter_context(tc.tile_pool(name="codes", bufs=9))
        dots_psum = ctx.enter_context(tc.psum_pool(name="dots_psum", bufs=3))
        et_psum = ctx.enter_context(tc.psum_pool(name="et_psum", bufs=2))
        o_psum = ctx.enter_context(tc.psum_pool(name="o_psum", bufs=1))
        prep_psum = ctx.enter_context(tc.psum_pool(name="prep_psum", bufs=2))

        q_sb, k_sb, hs_sb = [], [], []

        def load_qk(n):
            k_sb.append(loads.tile([P, H, TILES, D], BF16, name="k_sb"))
            q_sb.append(loads.tile([P, H, TILES, D], BF16, name="q_sb"))
            for h in range(H):
                for rows, rows_sb in ((k_rows, k_sb[n]), (q_rows, q_sb[n])):
                    row = h * S + n * CHUNK
                    nc.sync.dma_start(
                        out=rows_sb[:, h],
                        in_=rows[row : row + CHUNK, :].rearrange("(t p) d -> p t d", p=P),
                    )

        def load_hs(n):
            hs_sb.append(loads.tile([P, TILES, HID], BF16, name="hs_sb"))
            nc.sync.dma_start(
                out=hs_sb[n][:],
                in_=hs_rows[n * CHUNK : (n + 1) * CHUNK, :].rearrange("(p t) k -> p t k", t=PACK),
            )

        load_qk(0)
        load_qk(1)
        load_hs(0)
        wv_raw = const.tile([P, PASSES, PACK, H * D], BF16)
        nc.sync.dma_start(
            out=wv_raw[:].rearrange("p g (u e) c -> p (g u) (e c)", u=PLANES, e=2),
            in_=Wv.rearrange("(g u p e) c -> p (g u) (e c)", g=PASSES, u=PLANES, e=2),
        )
        load_hs(1)
        load_qk(2)
        load_hs(2)

        ident_bf = const.tile([P, P], BF16)
        make_identity(nc, ident_bf[:])
        ident_f32 = const.tile([P, P], F32)
        make_identity(nc, ident_f32[:])
        causal_f32 = const.tile([P, P], F32)
        nc.gpsimd.memset(causal_f32[:], 0.0)
        nc.gpsimd.affine_select(
            out=causal_f32[:],
            in_=causal_f32[:],
            pattern=[[-1, P]],
            compare_op=ALU.is_ge,
            fill=MASK_VALUE,
            base=0,
            channel_multiplier=1,
        )
        causal = const.tile([P, P], BF16)
        nc.vector.tensor_copy(
            out=causal[:].rearrange("p (u x e) -> p u x e", u=PLANES, e=2),
            in_=causal_f32[:].rearrange("p (x u e) -> p u x e", u=PLANES, e=2),
        )

        e_sb = [
            keep.tile([P, PLANES, QUARTERS * (1 + len(group)), RUN], BF16, name="e_sb_%d" % g)
            for g, group in enumerate(GROUPS)
        ]

        wv_codes = const.tile([P, PASSES, H * D], U32, align_bytes=64)
        wv_scales = const.tile([P, PASSES, H * D], U8, align_bytes=64)

        def wv_quantise():
            wv_grp = const.tile([P, PASSES, H * D, PACK], BF16, align_bytes=64)
            nc.gpsimd.tensor_scalar(
                out=wv_grp[:],
                in0=wv_raw[:].rearrange("p g t c -> p g c t"),
                scalar1=1.0,
                scalar2=0.0,
                op0=ALU.mult,
                op1=ALU.add,
            )
            nc.vector.quantize_mx(
                out=wv_codes[:].rearrange("p g c -> p (g c)").bitcast(FP8X4),
                scales=wv_scales[:].rearrange("p g c -> p (g c)"),
                in_=wv_grp[:].rearrange("p g c t -> p (g c t)"),
            )

        qT = [keep.tile([P, H, CHUNK], BF16, name="qT_%d" % n) for n in range(CHUNKS)]
        kT = [keep.tile([P, H, CHUNK], BF16, name="kT_%d" % n) for n in range(CHUNKS)]
        v_mx = [
            keep.tile([P, V_WORDS + V_WORDS // PACK], U32, align_bytes=64, name="v_mx_%d" % n)
            for n in range(CHUNKS)
        ]
        v_kept, v_moved = {}, {}
        for q in (1, 2):
            for i in range(2):
                v_kept[(q, i)] = keep.tile([P, V_WORDS], U32, align_bytes=64, name="v_kept_%d_%d" % (q, i))
                v_moved[(q, i)] = keep.tile(
                    [P, V_WORDS + V_WORDS // PACK], U32, align_bytes=64, name="v_moved_%d_%d" % (q, i)
                )
                nc.gpsimd.memset(v_kept[(q, i)][:].bitcast(I32), 0)
                nc.gpsimd.memset(v_moved[(q, i)][:].bitcast(I32), 0)

        def v_words(tile, h):
            return tile[:, h * D : (h + 1) * D].bitcast(FP8X4)

        def v_scale_bytes(tile, h):
            return tile[:, V_WORDS:].bitcast(U8)[:, h * D : (h + 1) * D]

        live = {}

        def prep_bank(shape, dtype):
            return prep_psum.tile(shape, dtype, tag="prep", name="prep_bank")

        def qk_flip(c, which, rows_sb, heads):
            flipped = prep_bank([P, len(heads), CHUNK], BF16)
            for at, h in enumerate(heads):
                for t in range(TILES):
                    nc.tensor.transpose(
                        flipped[:, at, t * P : (t + 1) * P], rows_sb[:, h, t, :], ident_bf[:]
                    )
            live[("flipped", c, which, heads)] = flipped

        def q_copy(c, heads, copy):
            copy(
                out=qT[c][:, heads.start : heads.stop].rearrange("p h s -> p (h s)").bitcast(F32),
                in_=live[("flipped", c, "q", heads)][:].rearrange("p h s -> p (h s)").bitcast(F32),
            )

        def k_copy(c, heads, copy):
            copy(
                out=kT[c][:, heads.start : heads.stop].rearrange("p h s -> p (h s)").bitcast(F32).rearrange(
                    "p (a u x) -> p a u x", u=PLANES, x=RUN // 2
                ),
                in_=live[("flipped", c, "k", heads)][:].rearrange("p h s -> p (h s)").bitcast(F32).rearrange(
                    "p (a x u) -> p a u x", u=PLANES, x=RUN // 2
                ),
            )

        hs_codes = [
            keep.tile([P, TILES, PASSES, P], U32, align_bytes=64, name="hs_codes_%d" % i) for i in range(2)
        ]
        hs_scales = [
            keep.tile([P, TILES, PASSES, P], U8, align_bytes=64, name="hs_scales_%d" % i) for i in range(2)
        ]
        v_grp = [keep.tile([P, H, D, PACK], BF16, align_bytes=64, name="v_grp_%d" % i) for i in range(2)]

        def hs_flip(c, t):
            hs_words = hs_sb[c][:, t, :].bitcast(F32)
            planes = prep_bank([P, PASSES * PLANES, P], F32)
            for b in range(PASSES * PLANES):
                nc.tensor.transpose(planes[:, b, :], hs_words[:, b * P : (b + 1) * P], ident_f32[:])
            live[("hs_planes", c, t)] = planes

        def hs_gather(c, t):
            hs_grp = work.tile([P, PASSES * CHUNK], BF16, align_bytes=64)
            nc.scalar.copy(
                out=hs_grp[:].bitcast(F32).rearrange("p (g r u) -> p g r u", g=PASSES, u=PLANES),
                in_=live[("hs_planes", c, t)][:].rearrange("p (g u) r -> p g r u", u=PLANES),
            )
            live[("hs_grp", c, t)] = hs_grp

        def hs_quantise(c, t):
            nc.vector.quantize_mx(
                out=hs_codes[c % 2][:, t].rearrange("p g r -> p (g r)").bitcast(FP8X4),
                scales=hs_scales[c % 2][:, t].rearrange("p g r -> p (g r)"),
                in_=live[("hs_grp", c, t)][:],
            )

        def v_project(c, h):
            v_ps = prep_bank([P, TILES, D], F32)
            for t in range(TILES):
                for g in range(PASSES):
                    nc.tensor.matmul_mx(
                        out=v_ps[:, t, :],
                        lhsT=hs_codes[c % 2][:, t, g, :].bitcast(FP8X4),
                        lhsT_scale=hs_scales[c % 2][:, t, g, :],
                        rhs=wv_codes[:, g, h * D : (h + 1) * D].bitcast(FP8X4),
                        rhs_scale=wv_scales[:, g, h * D : (h + 1) * D],
                        start=(g == 0),
                        stop=(g == PASSES - 1),
                    )
            live[("v_ps", c, h)] = v_ps

        def v_gather(c, h):
            copy = nc.vector.tensor_copy if h == 0 else nc.scalar.copy
            copy(out=v_grp[c % 2][:, h], in_=live[("v_ps", c, h)][:].rearrange("p t d -> p d t"))

        def v_quantise(c):
            nc.vector.quantize_mx(
                out=v_mx[c][:, :V_WORDS].bitcast(FP8X4),
                scales=v_mx[c][:, V_WORDS:].bitcast(U8),
                in_=v_grp[c % 2][:].rearrange("p h d t -> p (h d t)"),
            )

        def v_share(c):
            for q in (1, 2):
                kept, moved, border = v_kept[(q, c % 2)], v_moved[(q, c % 2)], q * QUADRANT
                nc.sync.dma_start(
                    out=kept[:border, :].bitcast(I32), in_=v_mx[c][:border, :V_WORDS].bitcast(I32)
                )
                nc.sync.dma_start(
                    out=moved[border:, :].bitcast(I32), in_=v_mx[c][: P - border, :].bitcast(I32)
                )

        def unit(u):
            g, place = ORDER[u % STEPS]
            return (u // STEPS,) + GROUPS[g][place]

        def is_second(u):
            return ORDER[u % STEPS][1] == 1

        def is_first(u):
            g, place = ORDER[u % STEPS]
            return place == 0 and len(GROUPS[g]) == 2

        def slots(u):
            n, j, h = unit(u)
            own = QUARTERS + (QUARTERS - 1 - j if is_second(u) else 0)
            first, last = own, own + j + 1
            if n > 0 and is_second(u):
                last += QUARTERS
            elif n > 0:
                first -= QUARTERS
            return slice(first, last)

        def passes(u):
            n, j, h = unit(u)
            if is_first(u):
                return range(0, 1 if n > 0 else 0)
            if is_second(u):
                return range(1, 3 if n > 0 else 2)
            return range(0 if n > 0 else 1, 2)

        def parts(u):
            if u == LAST:
                return [slice(0, QUARTERS), slice(QUARTERS, 2 * QUARTERS)]
            return [slots(u)]

        def runs(u):
            if u == LAST:
                return [range(s, s + 1) for s in passes(u)]
            return [passes(u)]

        def scores(u):
            n, j, h = unit(u)
            q_cols = qT[n][:, h, j * P : (j + 1) * P]
            seen = (j + 1) * P
            if n > 0:
                before = dots_psum.tile([P, CHUNK], F32, tag="dots")
                nc.tensor.matmul(out=before[:], lhsT=q_cols, rhs=kT[n - 1][:, h, :], start=True, stop=True)
                live[("before", u)] = before
            own = dots_psum.tile([P, CHUNK], F32, tag="dots")
            if j > 0:
                nc.tensor.matmul(
                    out=own[:, : j * P], lhsT=q_cols, rhs=kT[n][:, h, : j * P], start=True, stop=True
                )
            nc.tensor.matmul(
                out=own[:, j * P : seen], lhsT=q_cols, rhs=kT[n][:, h, j * P : seen], start=True, stop=False
            )
            nc.tensor.matmul(out=own[:, j * P : seen], lhsT=ident_bf[:], rhs=causal[:], start=False, stop=True)
            live[("own", u)] = own[:, :seen]
            minus_dots = work.tile([P, 2 * CHUNK], F32, name="minus_dots")
            own_at = CHUNK if n > 0 and not is_second(u) else 0
            before_at = seen if is_second(u) else 0
            live[("minus_own", u)] = minus_dots[:, own_at : own_at + seen]
            live[("minus_before", u)] = minus_dots[:, before_at : before_at + CHUNK]
            live[("minus_dots", u)] = minus_dots[:, : seen + (CHUNK if n > 0 else 0)]
            live[("lows", u)] = small.tile([P, 2], F32, name="lows")

        def move_before(u):
            nc.vector.tensor_scalar(
                out=live[("minus_before", u)],
                in0=live[("before", u)][:],
                scalar1=-1.0,
                scalar2=None,
                op0=ALU.mult,
                op1=ALU.min,
                accum_out=live[("lows", u)][:, 0:1],
            )

        def move_own(u):
            nc.vector.tensor_scalar(
                out=live[("minus_own", u)],
                in0=live[("own", u)],
                scalar1=-1.0,
                scalar2=live[("lows", u)][:, 0:1] if u >= STEPS else None,
                op0=ALU.mult,
                op1=ALU.min,
                accum_out=live[("lows", u)][:, 1:2],
            )

        def exponentials(u):
            bank, at = u // BANK_UNITS, column(u)
            if u % BANK_UNITS == 0:
                live[("sums", bank)] = small.tile([P, BANK_UNITS], F32, name="sums")
            if u == LAST:
                live["last_sum"] = small.tile([P, 1], F32, name="last_sum")
            for part in parts(u):
                columns = slice((part.start - slots(u).start) * P, (part.stop - slots(u).start) * P)
                nc.scalar.activation(
                    out=e_sb[ORDER[u % STEPS][0]][:, :, part, :].rearrange("p u s x -> p s u x"),
                    in_=live[("minus_dots", u)][:, columns].rearrange("p (s u x) -> p s u x", u=PLANES, x=RUN),
                    func=EXP,
                    bias=live[("lows", u)][:, 1:2],
                    scale=-1.0,
                    accum_out=(
                        live[("sums", bank)][:, at : at + 1]
                        if part.start == slots(u).start
                        else live["last_sum"][:]
                    ),
                )

        def flip_e(u):
            e_words = e_sb[ORDER[u % STEPS][0]][:].rearrange("p u s x -> p u (s x)").bitcast(F32)
            for run in runs(u):
                eT = et_psum.tile([P, 2, PLANES, P], F32, tag="eT")
                for w, s in enumerate(run):
                    for b in range(PLANES):
                        nc.tensor.transpose(eT[:, w, b, :], e_words[:, b, s * P : (s + 1) * P], ident_f32[:])
                live[("eT", u, run)] = eT

        def gather_e(u):
            copy = nc.vector.tensor_copy if UNITS - 2 <= u < LAST else nc.scalar.copy
            for run in runs(u):
                count = len(run)
                e_grp = work.tile([P, 2 * CHUNK], BF16, align_bytes=64)
                copy(
                    out=e_grp[:, : count * CHUNK].bitcast(F32).rearrange(
                        "p (w r u) -> p w r u", w=count, u=PLANES
                    ),
                    in_=live[("eT", u, run)][:, :count].rearrange("p w u r -> p w r u"),
                )
                live[("e_grp", u, run)] = e_grp

        def quantise_e(u):
            for run in runs(u):
                count = len(run)
                e_codes = codes.tile([P, 2 * P], U32, align_bytes=64)
                e_scales = codes.tile([P, 2 * P], U8, align_bytes=64)
                nc.vector.quantize_mx(
                    out=e_codes[:, : count * P].bitcast(FP8X4),
                    scales=e_scales[:, : count * P],
                    in_=live[("e_grp", u, run)][:, : count * CHUNK],
                )
                for w, s in enumerate(run):
                    live[("e_pass", u, s)] = (
                        e_codes[:, w * P : (w + 1) * P],
                        e_scales[:, w * P : (w + 1) * P],
                    )

        def column(u):
            n, j, h = unit(u)
            return j // 2 * H + h

        def product(u, last):
            n, j, h = unit(u)
            bank = u // BANK_UNITS
            if u % BANK_UNITS == 0:
                if n + 1 < CHUNKS:
                    live[("o_ps", bank)] = o_psum.tile([P, BANK_UNITS, D], F32, tag="o", name="o_ps")
                else:
                    live[("o_ps", bank)] = prep_bank([P, BANK_UNITS, D], F32)
            o_ps, at = live[("o_ps", bank)], column(u)
            if u == LAST:
                live["last_o_ps"] = o_psum.tile([P, BANK_UNITS, D], F32, tag="o", name="o_ps")
                o_ps = live["last_o_ps"]
            factors = []
            if n > 0:
                before = live[("e_pass", u, 2 if is_second(u) else 0)]
                factors.append((before, (v_words(v_mx[n - 1], h), v_scale_bytes(v_mx[n - 1], h))))
            if is_first(u):
                v_own = (v_words(v_kept[(j + 1, n % 2)], h), v_scale_bytes(v_mx[n], h))
            elif is_second(u):
                moved = v_moved[(QUARTERS - 1 - j, n % 2)]
                v_own = (v_words(moved, h), v_scale_bytes(moved, h))
            else:
                v_own = (v_words(v_mx[n], h), v_scale_bytes(v_mx[n], h))
            factors.append((live[("e_pass", last, 1)], v_own))
            for w, (e_side, v_side) in enumerate(factors):
                nc.tensor.matmul_mx(
                    out=o_ps[:, at, :],
                    lhsT=e_side[0].bitcast(FP8X4),
                    lhsT_scale=e_side[1],
                    rhs=v_side[0],
                    rhs_scale=v_side[1],
                    start=(w == 0),
                    stop=(w == len(factors) - 1),
                )

        def invert_sums(bank, columns):
            if columns.stop == BANK_UNITS and bank == LAST // BANK_UNITS:
                last = live[("sums", bank)][:, BANK_UNITS - 1 :]
                nc.vector.tensor_tensor(out=last, in0=last, in1=live["last_sum"][:], op=ALU.add)
            inverse = small.tile([P, BANK_UNITS], F32)
            nc.vector.reciprocal(out=inverse[:, columns], in_=live[("sums", bank)][:, columns])
            live[("inverse", bank)] = inverse

        def divide_and_store(bank, columns):
            count = columns.stop - columns.start
            o_sb = work.tile([P, BANK_UNITS, D], F32)
            nc.vector.tensor_tensor(
                out=o_sb[:, columns],
                in0=(live["last_o_ps"] if columns == finished(LAST) else live[("o_ps", bank)])[:, columns],
                in1=live[("inverse", bank)][:, columns].unsqueeze(2).to_broadcast([P, count, D]),
                op=ALU.mult,
            )
            n, x = bank // 2, bank % 2
            rows = out_rows[n * CHUNK : (n + 1) * CHUNK, :].rearrange("(a x p) c -> x p a c", a=2, x=2)[x]
            if count == BANK_UNITS:
                nc.sync.dma_start(out=rows, in_=o_sb[:].rearrange("p (a h) d -> p a (h d)", a=2))
            else:
                for at in range(columns.start, columns.stop):
                    nc.sync.dma_start(
                        out=rows[:, at // H, at % H * D : (at % H + 1) * D], in_=o_sb[:, at, :]
                    )

        def finished(u):
            if u == LAST:
                return slice(BANK_UNITS - 1, BANK_UNITS)
            if u == LAST - 1:
                return slice(0, BANK_UNITS - 1)
            return slice(0, BANK_UNITS) if u % BANK_UNITS == BANK_UNITS - 1 else None

        K_STEP, Q_STEP, HS_STEP, V_STEP = 0, 1, 2, 2 + TILES

        def exists(u):
            return 0 <= u < UNITS

        TABLE = (
            (1, HS_STEP + 3), (1, K_STEP), (1, Q_STEP), (1, V_STEP),
            (2, HS_STEP), (2, HS_STEP + 1), (2, HS_STEP + 2), (1, V_STEP + 1),
        )
        HEAD = {1: ((0, HS_STEP + 0),), 2: ((0, HS_STEP + 1),), 3: ((0, HS_STEP + 2),), 4: ((0, HS_STEP + 3),), 5: ((0, V_STEP + 0), (1, HS_STEP + 0),), 6: ((0, V_STEP + 1), (1, HS_STEP + 1),), 7: ((1, HS_STEP + 2),), 8: ((1, HS_STEP + 3),), 9: ((1, V_STEP + 0), (2, K_STEP),), 10: ((1, V_STEP + 1), (2, Q_STEP),), 11: ((2, HS_STEP + 0),), 12: ((2, HS_STEP + 1),), 13: ((2, HS_STEP + 2),), 14: ((2, HS_STEP + 3),), 15: ((2, V_STEP + 0), (3, K_STEP),), 16: ((2, V_STEP + 1), (3, Q_STEP),), 17: ((3, HS_STEP + 0),), 18: ((3, HS_STEP + 1),), 19: ((3, HS_STEP + 2),), 20: ((3, HS_STEP + 3),), 21: ((3, V_STEP + 0), (4, HS_STEP + 0),), 22: ((4, HS_STEP + 1),), 23: ((3, V_STEP + 1), (4, HS_STEP + 2),), -3: ((1, K_STEP),), -2: ((1, Q_STEP),)}

        def steps_of(i):
            steps = list(HEAD.get(i, ()))
            if i >= 24:
                ahead, step = TABLE[i % STEPS]
                if i // STEPS + ahead < CHUNKS:
                    steps.append((i // STEPS + ahead, step))
            return steps

        zeros = const.tile([P, CHUNK], BF16)
        nc.vector.memset(zeros[:], 0.0)

        def warm_up(count):
            idle = dots_psum.tile([P, CHUNK], F32, tag="dots", name="idle")
            for repeat in range(count):
                nc.tensor.matmul(out=idle[:], lhsT=zeros[:, :P], rhs=zeros[:], start=True, stop=True)

        def do_flip(c, step):
            if step == K_STEP:
                qk_flip(c, "k", k_sb[c], range(H))
            elif step == Q_STEP:
                qk_flip(c, "q", q_sb[c], range(H))
            elif step < V_STEP:
                hs_flip(c, step - HS_STEP)

        def do_copy(c, step):
            if step == K_STEP:
                k_copy(c, range(H), nc.scalar.copy)
            elif step == Q_STEP:
                q_copy(c, range(H), nc.vector.tensor_copy if c < 2 else nc.scalar.copy)
            elif step < V_STEP:
                hs_gather(c, step - HS_STEP)

        def tick(i):
            if exists(i):
                exponentials(i)
            if exists(i - 2) and passes(i - 2):
                gather_e(i - 2)
            if STEPS <= i + 4 < UNITS:
                move_before(i + 4)
            if exists(i - 1) and passes(i - 1):
                flip_e(i - 1)
            for c, step in steps_of(i):
                do_flip(c, step)
            if exists(i + 5):
                scores(i + 5)
            elif 0 < i < UNITS:
                warm_up(2)
            if exists(i - 3) and passes(i - 3):
                quantise_e(i - 3)
            if exists(i - 10) and finished(i - 10):
                divide_and_store((i - 10) // BANK_UNITS, finished(i - 10))
            if exists(i + 4):
                move_own(i + 4)
            for c, step in steps_of(i - 1):
                if step >= V_STEP:
                    v_gather(c, step - V_STEP)
            for c, step in steps_of(i - 1):
                if HS_STEP <= step < V_STEP:
                    hs_quantise(c, step - HS_STEP)
            for c, step in steps_of(i - 2):
                if step == STEPS - 1:
                    v_quantise(c)
                    v_share(c)
            if i >= 0 and i % STEPS == STEPS // 2 and i // STEPS + 3 < CHUNKS:
                load_qk(i // STEPS + 3)
                load_hs(i // STEPS + 3)
            if i == 3:
                wv_quantise()
            for c, step in steps_of(i):
                if step >= V_STEP:
                    v_project(c, step - V_STEP)
            if exists(i - 9):
                product(i - 9, i - 9 + (1 if is_first(i - 9) else 0))
            if exists(i - 9) and finished(i - 9):
                invert_sums((i - 9) // BANK_UNITS, finished(i - 9))
            for c, step in steps_of(i):
                do_copy(c, step)

        HEAD_TICKS = 4
        with tc.manual_schedule():
            warm_up(5)
            for h in range(H):
                qk_flip(0, "k", k_sb[0], range(h, h + 1))
                k_copy(0, range(h, h + 1), nc.scalar.copy)
                qk_flip(0, "q", q_sb[0], range(h, h + 1))
                q_copy(0, range(h, h + 1), nc.vector.tensor_copy)
            for i in range(-5, HEAD_TICKS):
                tick(i)
        for i in range(HEAD_TICKS, UNITS + 10 + 1):
            tick(i)
